import numpy as np
import ml_dtypes


def mxq(x, axis, fmt="e4m3"):
    dtype, down = {"e4m3": (ml_dtypes.float8_e4m3fn, 7), "e5m2": (ml_dtypes.float8_e5m2, 14)}[fmt]
    v = np.moveaxis(np.asarray(x, np.float32).astype(ml_dtypes.bfloat16).astype(np.float64), axis, -1)
    blocks = v.reshape(v.shape[:-1] + (-1, 32))
    amax = np.abs(blocks).max(-1, keepdims=True)
    byte = np.maximum(np.where(amax > 0, np.frexp(amax)[1] - 1 + 127, 0) - down, 1)
    scale = np.exp2(byte - 127.0)
    codes = (blocks / scale).astype(np.float32).astype(dtype).astype(np.float64)
    return np.moveaxis((codes * scale).reshape(v.shape), -1, axis)


WIDE = False


def mx_kscale(k):
    if not WIDE:
        return np.ones(k)
    levels = np.array([10, -10, 5, -5, 0])
    a = np.random.permutation(np.resize(levels, k // 512 * 4)).reshape(k // 512, 4)
    idx = np.arange(k)
    return np.exp2(a[idx // 512, idx % 128 // 32])


BF16 = ml_dtypes.bfloat16


def bf(x):
    return np.asarray(x, np.float32).astype(BF16)


def f64(x):
    return np.asarray(x).astype(np.float64)


E2M1 = np.array([0.0, 0.5, 1.0, 1.5, 2.0, 3.0, 4.0, 6.0, -0.0, -0.5, -1.0, -1.5, -2.0, -3.0, -4.0, -6.0])


def pack_weight(w, fmt):
    k, n = w.shape
    w = f64(bf(w)).reshape(k // 32, 32, n)
    amax = np.abs(w).max(1)
    if fmt == "e4m3":
        byte = np.frexp(amax)[1] - 1 + 127 - 7
    else:
        mant, ex = np.frexp(amax / 6.0)
        byte = np.where(mant > 0.5, ex, ex - 1) + 127
    byte = np.clip(np.where(amax > 0, byte, 1), 1, 254)
    scaled = (w * np.exp2(127.0 - byte)[:, None, :]).reshape(k, n).astype(np.float32)
    by_word = np.ascontiguousarray(scaled.reshape(k // 512, 128, 4, n).transpose(0, 1, 3, 2))
    if fmt == "e4m3":
        words = by_word.astype(ml_dtypes.float8_e4m3fn).view(np.uint8)
    else:
        c = by_word.astype(ml_dtypes.float4_e2m1fn).view(np.uint8) & 0xF
        words = c[..., 0::2] | (c[..., 1::2] << 4)
    return np.ascontiguousarray(words), np.ascontiguousarray(byte.astype(np.uint8).reshape(k // 512, 16, n))


def unpack_weight(words, scales, fmt):
    g, p, n, _ = words.shape
    if fmt == "e4m3":
        vals = np.ascontiguousarray(words).view(ml_dtypes.float8_e4m3fn).astype(np.float64)
    else:
        nib = np.empty((g, p, n, 4), np.uint8)
        nib[..., 0::2] = words & 0xF
        nib[..., 1::2] = words >> 4
        vals = E2M1[nib]
    vals = vals * np.repeat(np.exp2(scales.astype(np.float64) - 127.0), 8, axis=1)[..., None]
    return vals.transpose(0, 1, 3, 2).reshape(g * 512, n)


B, I, H, C, S = 128, 512, 512, 8191, 3
EPSILON = 1e-6
CC = 1 + C
K = I + H
FMT = "e4m3"


def setup_inputs():
    s = mx_kscale(K)
    t = mx_kscale(CC)
    t = t / t.min()
    invariant_input = bf(np.random.standard_normal((B, I)) * s[:I])
    equivariant_input = bf(np.random.standard_normal((B, S)) * 0.125 * t[0])
    invariant_hidden = bf(np.random.standard_normal((B, H)) * s[I:])
    equivariant_hidden = bf(np.random.standard_normal((B, S, C)) * 0.125 * t[1:])
    W_left_words, W_left_scales = pack_weight(np.random.standard_normal((CC, H)) * 0.15 / np.sqrt(CC) * t[:, None], FMT)
    W_right_words, W_right_scales = pack_weight(np.random.standard_normal((CC, H)) * 0.15 / np.sqrt(CC) * t[:, None], FMT)
    W_ii_words, W_ii_scales = pack_weight(np.random.standard_normal((K, H)) * 0.6 / np.sqrt(K) / s[:, None], FMT)
    b_ii = bf(np.random.standard_normal(H) * 0.3)
    return {
        "invariant_input": invariant_input,
        "equivariant_input": equivariant_input,
        "invariant_hidden": invariant_hidden,
        "equivariant_hidden": equivariant_hidden,
        "W_left_words": W_left_words,
        "W_left_scales": W_left_scales,
        "W_right_words": W_right_words,
        "W_right_scales": W_right_scales,
        "W_ii_words": W_ii_words,
        "W_ii_scales": W_ii_scales,
        "b_ii": b_ii,
    }


def reference(invariant_input, equivariant_input, invariant_hidden, equivariant_hidden, W_left_words, W_left_scales, W_right_words, W_right_scales, W_ii_words, W_ii_scales, b_ii):
    eq_comb = np.concatenate([f64(equivariant_input)[..., None], f64(equivariant_hidden)], axis=-1)
    inv_comb = np.concatenate([f64(invariant_input), f64(invariant_hidden)], axis=-1)
    norm = np.sum(eq_comb * eq_comb, axis=-2, keepdims=True) + EPSILON
    xn = mxq(eq_comb / norm, 2, "e4m3")
    left = xn @ unpack_weight(W_left_words, W_left_scales, FMT)
    right = xn @ unpack_weight(W_right_words, W_right_scales, FMT)
    proj = np.sum(left * right, axis=-2)
    lin = mxq(inv_comb, 1, "e4m3") @ unpack_weight(W_ii_words, W_ii_scales, FMT)
    return np.tanh(proj + lin + f64(b_ii))

@@ -1,0 +1,269 @@
+from contextlib import ExitStack
+
+import concourse.mybir as mybir
+from concourse.masks import make_identity
+
+F32 = mybir.dt.float32
+BF16 = mybir.dt.bfloat16
+I32 = mybir.dt.int32
+U32 = mybir.dt.uint32
+U8 = mybir.dt.uint8
+FP8X4 = mybir.dt.float8_e4m3fn_x4
+ACT = mybir.ActivationFunctionType
+ALU = mybir.AluOpType
+
+P = 128
+PACK = 4
+K_PASS = P * PACK
+PASS_WORDS = K_PASS // 2
+COMPONENTS = 3
+CHANNELS = 8192
+FEATURES = 1024
+H = 512
+EPSILON = 1e-6
+STEPS = CHANNELS // K_PASS
+II_PASSES = FEATURES // K_PASS
+BLOCK = 16
+SIDES = ("left", "right")
+EQ_LOADS = ((0, 1), (1, 1)) + tuple((first, 2) for first in range(2, STEPS, 2))
+
+FLOPS = 2 * P * COMPONENTS * CHANNELS * H * 2 + 2 * P * FEATURES * H
+
+
+def transpose_pass(nc, planes, words, identity):
+    for u in range(2):
+        nc.tensor.transpose(planes[:, u, :], words[:, u:PASS_WORDS:2], identity[:])
+
+
+def load_weight(nc, words_tile, words, first, count):
+    nc.sync.dma_start(
+        out=words_tile[:, first : first + count, :].bitcast(I32),
+        in_=words[first : first + count].rearrange("g p n t -> p g (n t)").bitcast(I32),
+    )
+
+
+def load_scales(nc, planes, scales):
+    by_quadrant = scales.rearrange("g (q r) n -> q r g n", r=4)
+    for q in range(4):
+        nc.sync.dma_start(out=planes[32 * q : 32 * q + 4, :, :].bitcast(I32), in_=by_quadrant[q].bitcast(I32))
+
+
+def tile_ryeelman_pa_k_kernel(
+    tc,
+    invariant_input,
+    equivariant_input,
+    invariant_hidden,
+    equivariant_hidden,
+    W_left_words,
+    W_left_scales,
+    W_right_words,
+    W_right_scales,
+    W_ii_words,
+    W_ii_scales,
+    b_ii,
+    out,
+):
+    nc = tc.nc
+    with ExitStack() as stack:
+        stack.enter_context(tc.manual_schedule())
+        keep = stack.enter_context(tc.tile_pool(name="keep", bufs=1))
+        turned = stack.enter_context(tc.tile_pool(name="turned", bufs=4))
+        work = stack.enter_context(tc.tile_pool(name="work", bufs=2))
+        packed = stack.enter_context(tc.tile_pool(name="packed", bufs=3))
+        accs = stack.enter_context(tc.psum_pool(name="accs", bufs=1))
+        banks = stack.enter_context(tc.psum_pool(name="banks", bufs=1))
+
+        identity = keep.tile([P, P], F32)
+        make_identity(nc, identity[:])
+
+        eq_tiles = {}
+        eq_home = {}
+        for first, count in EQ_LOADS:
+            eq_tiles[first] = keep.tile([P, COMPONENTS, count * K_PASS], BF16, align_bytes=64, name="eq_%d" % first)
+            for i in range(count):
+                eq_home[first + i] = (first, K_PASS * i)
+        one = keep.tile([P, 1], F32)
+        nc.vector.memset(one[:], 1.0)
+        warm = keep.tile([P, 2], F32)
+        nc.scalar.activation(out=warm[:, 0:1], in_=one[:], func=ACT.Abs_reciprocal_sqrt)
+        first_input = keep.tile([P, COMPONENTS], BF16)
+        first_hidden = keep.tile([P, COMPONENTS, BLOCK - 1], BF16)
+        inv = keep.tile([P, FEATURES], BF16, align_bytes=64)
+        bias = keep.tile([P, H], BF16)
+        w_words = {}
+        w_planes = {}
+        for side in SIDES:
+            w_words[side] = keep.tile([P, STEPS, PACK * H], U8, align_bytes=64, name="w_words_" + side)
+            w_planes[side] = keep.tile([P, STEPS, H], U8, align_bytes=64, name="w_planes_" + side)
+            nc.vector.memset(w_planes[side][:].bitcast(I32), 0)
+        ii_words = keep.tile([P, II_PASSES, PACK * H], U8, align_bytes=64)
+        ii_planes = keep.tile([P, II_PASSES, H], U8, align_bytes=64)
+        nc.vector.memset(ii_planes[:].bitcast(I32), 0)
+
+        def load_eq(first, skip):
+            lo = K_PASS * first
+            hi = lo + eq_tiles[first].shape[2]
+            nc.sync.dma_start(out=eq_tiles[first][:, :, skip:], in_=equivariant_hidden[:, :, lo + skip - 1 : hi - 1])
+
+        nc.sync.dma_start(out=first_input[:], in_=equivariant_input)
+        nc.sync.dma_start(out=first_hidden[:], in_=equivariant_hidden[:, :, 0 : BLOCK - 1])
+        load_eq(0, BLOCK)
+        load_eq(1, 0)
+        load_eq(2, 0)
+        load_scales(nc, w_planes["left"], W_left_scales)
+        load_scales(nc, w_planes["right"], W_right_scales)
+        for first in range(0, STEPS, 2):
+            load_weight(nc, w_words["left"], W_left_words, first, 2)
+            load_weight(nc, w_words["right"], W_right_words, first, 2)
+            if first + 4 < STEPS:
+                load_eq(first + 4, 0)
+        nc.sync.dma_start(out=inv[:, 0 : FEATURES // 2], in_=invariant_input)
+        nc.sync.dma_start(out=inv[:, FEATURES // 2 : FEATURES], in_=invariant_hidden)
+        load_weight(nc, ii_words, W_ii_words, 0, II_PASSES)
+        load_scales(nc, ii_planes, W_ii_scales)
+        nc.sync.dma_start(out=bias[:], in_=b_ii.partition_broadcast(P))
+
+        nc.vector.tensor_copy(out=eq_tiles[0][:, :, 0:1], in_=first_input[:].unsqueeze(2))
+        nc.vector.tensor_copy(out=eq_tiles[0][:, :, 1:BLOCK], in_=first_hidden[:])
+
+        acc = {}
+        for side in SIDES:
+            for j in range(COMPONENTS):
+                acc[side, j] = accs.tile([P, H], F32, name="acc_%s_%d" % (side, j))
+
+        pair_bank = {}
+        last_bank = {}
+        eq_t = {}
+        squares = {}
+        norm = {}
+        recip = {}
+        xn = {}
+        codes = {}
+        planes = {}
+
+        def turn_in(s):
+            pair_bank[s] = banks.tile([P, 2, 2, P], F32, name="pair_bank")
+            last_bank[s] = banks.tile([P, 2, P], F32, name="last_bank")
+            first, column = eq_home[s]
+            for j in range(COMPONENTS):
+                words = eq_tiles[first][:, j, column : column + K_PASS].bitcast(F32)
+                transpose_pass(nc, pair_bank[s][:, j] if j < 2 else last_bank[s][:], words, identity)
+
+        def turn_out(s):
+            eq_t[s] = turned.tile([P, COMPONENTS, P, PACK], BF16, align_bytes=64, name="eq_t")
+            nc.scalar.copy(out=eq_t[s][:, 0:2].bitcast(F32), in_=pair_bank[s][:].rearrange("p j u b -> p j b u"))
+            nc.vector.tensor_copy(out=eq_t[s][:, 2].bitcast(F32), in_=last_bank[s][:].rearrange("p u b -> p b u"))
+
+        def square(s):
+            squares[s] = work.tile([P, COMPONENTS, K_PASS], F32, name="squares")
+            nc.scalar.activation(out=squares[s][:], in_=eq_t[s][:].rearrange("p j b t -> p j (b t)"), func=ACT.Square)
+
+        def add_two(s):
+            norm[s] = work.tile([P, K_PASS], F32, name="norm")
+            nc.vector.scalar_tensor_tensor(
+                out=norm[s][:], in0=squares[s][:, 0, :], scalar=EPSILON, in1=squares[s][:, 1, :], op0=ALU.add, op1=ALU.add
+            )
+
+        def add_third(s):
+            nc.vector.tensor_tensor(out=norm[s][:], in0=norm[s][:], in1=squares[s][:, 2, :], op=ALU.add)
+
+        def root(s):
+            recip[s] = work.tile([P, K_PASS], F32, name="recip")
+            nc.scalar.activation(out=recip[s][:], in_=norm[s][:], func=ACT.Abs_reciprocal_sqrt)
+
+        def root_squared(s):
+            nc.scalar.activation(out=recip[s][:], in_=recip[s][:], func=ACT.Square)
+
+        def scale(s):
+            xn[s] = work.tile([P, COMPONENTS, K_PASS], BF16, align_bytes=64, name="xn")
+            nc.vector.tensor_tensor(
+                out=xn[s][:],
+                in0=eq_t[s][:].rearrange("p j b t -> p j (b t)"),
+                in1=recip[s][:].unsqueeze(1).to_broadcast([P, COMPONENTS, K_PASS]),
+                op=ALU.mult,
+            )
+
+        def quantise(s):
+            codes[s] = packed.tile([P, COMPONENTS, P], U32, align_bytes=64, name="codes")
+            planes[s] = packed.tile([P, COMPONENTS, P], U8, align_bytes=64, name="planes")
+            for j in range(COMPONENTS):
+                nc.vector.quantize_mx(out=codes[s][:, j, :].bitcast(FP8X4), scales=planes[s][:, j, :], in_=xn[s][:, j, :])
+
+        def contract(s):
+            for j in range(COMPONENTS):
+                for side in SIDES:
+                    nc.tensor.matmul_mx(
+                        out=acc[side, j][:],
+                        lhsT=codes[s][:, j, :].bitcast(FP8X4),
+                        lhsT_scale=planes[s][:, j, :],
+                        rhs=w_words[side][:, s, :].bitcast(FP8X4),
+                        rhs_scale=w_planes[side][:, s, :],
+                        start=(s == 0),
+                        stop=(s == STEPS - 1),
+                    )
+
+        def period(s):
+            if 0 <= s + 2 < STEPS:
+                square(s + 2)
+            if 0 <= s + 1 < STEPS:
+                root(s + 1)
+            if 0 <= s + 3 < STEPS:
+                turn_out(s + 3)
+            if s + 4 < STEPS:
+                turn_in(s + 4)
+            if 0 <= s + 1 < STEPS:
+                root_squared(s + 1)
+            if 0 <= s:
+                scale(s)
+            if 0 <= s + 2 < STEPS:
+                add_two(s + 2)
+            if 0 <= s:
+                quantise(s)
+            if 0 <= s + 2 < STEPS:
+                add_third(s + 2)
+            if 0 <= s:
+                contract(s)
+
+        turn_in(0)
+        for s in range(-3, STEPS - 3):
+            period(s)
+
+        inv_bank = banks.tile([P, II_PASSES, 2, P], F32, name="pair_bank")
+        for c in range(II_PASSES):
+            transpose_pass(nc, inv_bank[:, c], inv[:, K_PASS * c : K_PASS * (c + 1)].bitcast(F32), identity)
+        inv_t = keep.tile([P, II_PASSES, P, PACK], BF16, align_bytes=64)
+        nc.scalar.copy(out=inv_t[:].bitcast(F32), in_=inv_bank[:].rearrange("p c u b -> p c b u"))
+        inv_codes = keep.tile([P, II_PASSES, P], U32, align_bytes=64)
+        inv_planes = keep.tile([P, II_PASSES, P], U8, align_bytes=64)
+        nc.vector.quantize_mx(
+            out=inv_codes[:].rearrange("p c b -> p (c b)").bitcast(FP8X4),
+            scales=inv_planes[:].rearrange("p c b -> p (c b)"),
+            in_=inv_t[:].rearrange("p c b t -> p (c b t)"),
+        )
+        lin = banks.tile([P, H], F32, name="last_bank")
+        for c in range(II_PASSES):
+            nc.tensor.matmul_mx(
+                out=lin[:],
+                lhsT=inv_codes[:, c, :].bitcast(FP8X4),
+                lhsT_scale=inv_planes[:, c, :],
+                rhs=ii_words[:, c, :].bitcast(FP8X4),
+                rhs_scale=ii_planes[:, c, :],
+                start=(c == 0),
+                stop=(c == II_PASSES - 1),
+            )
+
+        for s in range(STEPS - 3, STEPS):
+            period(s)
+
+        nc.scalar.activation(out=warm[:, 1:2], in_=one[:], func=ACT.Tanh)
+        total = keep.tile([P, H], F32)
+        nc.vector.tensor_tensor(out=total[:], in0=lin[:], in1=bias[:], op=ALU.add)
+        for j in range(COMPONENTS):
+            left = keep.tile([P, H], F32, name="left_%d" % j)
+            nc.scalar.copy(out=left[:], in_=acc["left", j][:])
+            product = keep.tile([P, H], F32, name="product_%d" % j)
+            nc.vector.tensor_tensor(out=product[:], in0=left[:], in1=acc["right", j][:], op=ALU.mult)
+            nc.vector.tensor_tensor(out=total[:], in0=total[:], in1=product[:], op=ALU.add)
+        result = keep.tile([P, H], F32)
+        nc.scalar.activation(out=result[:], in_=total[:], func=ACT.Tanh)
+        nc.sync.dma_start(out=out, in_=result[:])

@@ -110,13 +110,14 @@ def tile_ryeelman_pa_k_kernel(
         load_eq(0, BLOCK)
         load_eq(1, 0)
         load_eq(2, 0)
+        load_eq(4, 0)
         load_scales(nc, w_planes["left"], W_left_scales)
         load_scales(nc, w_planes["right"], W_right_scales)
         for first in range(0, STEPS, 2):
             load_weight(nc, w_words["left"], W_left_words, first, 2)
             load_weight(nc, w_words["right"], W_right_words, first, 2)
-            if first + 4 < STEPS:
-                load_eq(first + 4, 0)
+            if first + 6 < STEPS:
+                load_eq(first + 6, 0)
         nc.sync.dma_start(out=inv[:, 0 : FEATURES // 2], in_=invariant_input)
         nc.sync.dma_start(out=inv[:, FEATURES // 2 : FEATURES], in_=invariant_hidden)
         load_weight(nc, ii_words, W_ii_words, 0, II_PASSES)

@@ -24,6 +24,7 @@ EPSILON = 1e-6
 STEPS = CHANNELS // K_PASS
 II_PASSES = FEATURES // K_PASS
 BLOCK = 16
+SHARE = 4
 SIDES = ("left", "right")
 EQ_LOADS = ((0, 1), (1, 1)) + tuple((first, 2) for first in range(2, STEPS, 2))
 
@@ -42,10 +43,12 @@ def load_weight(nc, words_tile, words, first, count):
     )
 
 
-def load_scales(nc, planes, scales):
-    by_quadrant = scales.rearrange("g (q r) n -> q r g n", r=4)
+def load_scales(nc, shared, scales):
+    count = scales.shape[0]
     for q in range(4):
-        nc.sync.dma_start(out=planes[32 * q : 32 * q + 4, :, :].bitcast(I32), in_=by_quadrant[q].bitcast(I32))
+        nc.sync.dma_start(
+            out=shared[32 * q : 32 * q + 4 * count, :].bitcast(I32), in_=scales[:, 4 * q : 4 * q + 4, :].bitcast(I32)
+        )
 
 
 def tile_ryeelman_pa_k_kernel(
@@ -94,10 +97,10 @@ def tile_ryeelman_pa_k_kernel(
         w_planes = {}
         for side in SIDES:
             w_words[side] = keep.tile([P, STEPS, PACK * H], U8, align_bytes=64, name="w_words_" + side)
-            w_planes[side] = keep.tile([P, STEPS, H], U8, align_bytes=64, name="w_planes_" + side)
+            w_planes[side] = keep.tile([P, STEPS // SHARE, H], U8, align_bytes=64, name="w_planes_" + side)
             nc.vector.memset(w_planes[side][:].bitcast(I32), 0)
         ii_words = keep.tile([P, II_PASSES, PACK * H], U8, align_bytes=64)
-        ii_planes = keep.tile([P, II_PASSES, H], U8, align_bytes=64)
+        ii_planes = keep.tile([P, H], U8, align_bytes=64)
         nc.vector.memset(ii_planes[:].bitcast(I32), 0)
 
         def load_eq(first, skip):
@@ -111,9 +114,10 @@ def tile_ryeelman_pa_k_kernel(
         load_eq(1, 0)
         load_eq(2, 0)
         load_eq(4, 0)
-        load_scales(nc, w_planes["left"], W_left_scales)
-        load_scales(nc, w_planes["right"], W_right_scales)
         for first in range(0, STEPS, 2):
+            if first % SHARE == 0:
+                load_scales(nc, w_planes["left"][:, first // SHARE, :], W_left_scales[first : first + SHARE])
+                load_scales(nc, w_planes["right"][:, first // SHARE, :], W_right_scales[first : first + SHARE])
             load_weight(nc, w_words["left"], W_left_words, first, 2)
             load_weight(nc, w_words["right"], W_right_words, first, 2)
             if first + 6 < STEPS:
@@ -121,7 +125,7 @@ def tile_ryeelman_pa_k_kernel(
         nc.sync.dma_start(out=inv[:, 0 : FEATURES // 2], in_=invariant_input)
         nc.sync.dma_start(out=inv[:, FEATURES // 2 : FEATURES], in_=invariant_hidden)
         load_weight(nc, ii_words, W_ii_words, 0, II_PASSES)
-        load_scales(nc, ii_planes, W_ii_scales)
+        load_scales(nc, ii_planes[:], W_ii_scales)
         nc.sync.dma_start(out=bias[:], in_=b_ii.partition_broadcast(P))
 
         nc.vector.tensor_copy(out=eq_tiles[0][:, :, 0:1], in_=first_input[:].unsqueeze(2))
@@ -198,7 +202,7 @@ def tile_ryeelman_pa_k_kernel(
                         lhsT=codes[s][:, j, :].bitcast(FP8X4),
                         lhsT_scale=planes[s][:, j, :],
                         rhs=w_words[side][:, s, :].bitcast(FP8X4),
-                        rhs_scale=w_planes[side][:, s, :],
+                        rhs_scale=w_planes[side][4 * (s % SHARE) : P, s // SHARE, :],
                         start=(s == 0),
                         stop=(s == STEPS - 1),
                     )
@@ -248,7 +252,7 @@ def tile_ryeelman_pa_k_kernel(
                 lhsT=inv_codes[:, c, :].bitcast(FP8X4),
                 lhsT_scale=inv_planes[:, c, :],
                 rhs=ii_words[:, c, :].bitcast(FP8X4),
-                rhs_scale=ii_planes[:, c, :],
+                rhs_scale=ii_planes[4 * c : P, :],
                 start=(c == 0),
                 stop=(c == II_PASSES - 1),
             )

@@ -24,6 +24,7 @@ EPSILON = 1e-6
 STEPS = CHANNELS // K_PASS
 II_PASSES = FEATURES // K_PASS
 BLOCK = 16
+VECTOR_COPIES = 4
 SHARE = 4
 SIDES = ("left", "right")
 EQ_LOADS = ((0, 1), (1, 1)) + tuple((first, 2) for first in range(2, STEPS, 2))
@@ -156,8 +157,9 @@ def tile_ryeelman_pa_k_kernel(
 
         def turn_out(s):
             eq_t[s] = turned.tile([P, COMPONENTS, P, PACK], BF16, align_bytes=64, name="eq_t")
-            nc.scalar.copy(out=eq_t[s][:, 0:2].bitcast(F32), in_=pair_bank[s][:].rearrange("p j u b -> p j b u"))
-            nc.vector.tensor_copy(out=eq_t[s][:, 2].bitcast(F32), in_=last_bank[s][:].rearrange("p u b -> p b u"))
+            copy = nc.vector.tensor_copy if s < VECTOR_COPIES else nc.scalar.copy
+            copy(out=eq_t[s][:, 0:2].bitcast(F32), in_=pair_bank[s][:].rearrange("p j u b -> p j b u"))
+            copy(out=eq_t[s][:, 2].bitcast(F32), in_=last_bank[s][:].rearrange("p u b -> p b u"))
 
         def square(s):
             squares[s] = work.tile([P, COMPONENTS, K_PASS], F32, name="squares")

@@ -23,21 +23,25 @@ H = 512
 EPSILON = 1e-6
 STEPS = CHANNELS // K_PASS
 II_PASSES = FEATURES // K_PASS
-BLOCK = 16
-VECTOR_COPIES = 4
-SHARE = 4
 SIDES = ("left", "right")
+BLOCK = 16
+SHARE = 4
 EQ_LOADS = ((0, 1), (1, 1)) + tuple((first, 2) for first in range(2, STEPS, 2))
+TRANSPOSE_AHEAD = 4
+COPY_AHEAD = 3
+SQUARE_AHEAD = 2
+ROOT_AHEAD = 1
+FILL_STEPS = COPY_AHEAD + 1
 
 FLOPS = 2 * P * COMPONENTS * CHANNELS * H * 2 + 2 * P * FEATURES * H
 
 
-def transpose_pass(nc, planes, words, identity):
+def transpose_pass(nc, halves, words, identity):
     for u in range(2):
-        nc.tensor.transpose(planes[:, u, :], words[:, u:PASS_WORDS:2], identity[:])
+        nc.tensor.transpose(halves[:, u, :], words[:, u:PASS_WORDS:2], identity[:])
 
 
-def load_weight(nc, words_tile, words, first, count):
+def load_words(nc, words_tile, words, first, count):
     nc.sync.dma_start(
         out=words_tile[:, first : first + count, :].bitcast(I32),
         in_=words[first : first + count].rearrange("g p n t -> p g (n t)").bitcast(I32),
@@ -71,14 +75,19 @@ def tile_ryeelman_pa_k_kernel(
     with ExitStack() as stack:
         stack.enter_context(tc.manual_schedule())
         keep = stack.enter_context(tc.tile_pool(name="keep", bufs=1))
-        turned = stack.enter_context(tc.tile_pool(name="turned", bufs=4))
+        turned = stack.enter_context(tc.tile_pool(name="turned", bufs=COPY_AHEAD + 1))
         work = stack.enter_context(tc.tile_pool(name="work", bufs=2))
         packed = stack.enter_context(tc.tile_pool(name="packed", bufs=3))
-        accs = stack.enter_context(tc.psum_pool(name="accs", bufs=1))
+        sums = stack.enter_context(tc.psum_pool(name="sums", bufs=1))
         banks = stack.enter_context(tc.psum_pool(name="banks", bufs=1))
 
         identity = keep.tile([P, P], F32)
         make_identity(nc, identity[:])
+
+        one = keep.tile([P, 1], F32)
+        nc.vector.memset(one[:], 1.0)
+        warm = keep.tile([P, 2], F32)
+        nc.scalar.activation(out=warm[:, 0:1], in_=one[:], func=ACT.Abs_reciprocal_sqrt)
 
         eq_tiles = {}
         eq_home = {}
@@ -86,10 +95,6 @@ def tile_ryeelman_pa_k_kernel(
             eq_tiles[first] = keep.tile([P, COMPONENTS, count * K_PASS], BF16, align_bytes=64, name="eq_%d" % first)
             for i in range(count):
                 eq_home[first + i] = (first, K_PASS * i)
-        one = keep.tile([P, 1], F32)
-        nc.vector.memset(one[:], 1.0)
-        warm = keep.tile([P, 2], F32)
-        nc.scalar.activation(out=warm[:, 0:1], in_=one[:], func=ACT.Abs_reciprocal_sqrt)
         first_input = keep.tile([P, COMPONENTS], BF16)
         first_hidden = keep.tile([P, COMPONENTS, BLOCK - 1], BF16)
         inv = keep.tile([P, FEATURES], BF16, align_bytes=64)
@@ -99,10 +104,10 @@ def tile_ryeelman_pa_k_kernel(
         for side in SIDES:
             w_words[side] = keep.tile([P, STEPS, PACK * H], U8, align_bytes=64, name="w_words_" + side)
             w_planes[side] = keep.tile([P, STEPS // SHARE, H], U8, align_bytes=64, name="w_planes_" + side)
-            nc.vector.memset(w_planes[side][:].bitcast(I32), 0)
         ii_words = keep.tile([P, II_PASSES, PACK * H], U8, align_bytes=64)
         ii_planes = keep.tile([P, H], U8, align_bytes=64)
-        nc.vector.memset(ii_planes[:].bitcast(I32), 0)
+        for plane_tile in (w_planes["left"], w_planes["right"], ii_planes):
+            nc.vector.memset(plane_tile[:].bitcast(I32), 0)
 
         def load_eq(first, skip):
             lo = K_PASS * first
@@ -119,13 +124,13 @@ def tile_ryeelman_pa_k_kernel(
             if first % SHARE == 0:
                 load_scales(nc, w_planes["left"][:, first // SHARE, :], W_left_scales[first : first + SHARE])
                 load_scales(nc, w_planes["right"][:, first // SHARE, :], W_right_scales[first : first + SHARE])
-            load_weight(nc, w_words["left"], W_left_words, first, 2)
-            load_weight(nc, w_words["right"], W_right_words, first, 2)
+            load_words(nc, w_words["left"], W_left_words, first, 2)
+            load_words(nc, w_words["right"], W_right_words, first, 2)
             if first + 6 < STEPS:
                 load_eq(first + 6, 0)
         nc.sync.dma_start(out=inv[:, 0 : FEATURES // 2], in_=invariant_input)
         nc.sync.dma_start(out=inv[:, FEATURES // 2 : FEATURES], in_=invariant_hidden)
-        load_weight(nc, ii_words, W_ii_words, 0, II_PASSES)
+        load_words(nc, ii_words, W_ii_words, 0, II_PASSES)
         load_scales(nc, ii_planes[:], W_ii_scales)
         nc.sync.dma_start(out=bias[:], in_=b_ii.partition_broadcast(P))
 
@@ -135,53 +140,63 @@ def tile_ryeelman_pa_k_kernel(
         acc = {}
         for side in SIDES:
             for j in range(COMPONENTS):
-                acc[side, j] = accs.tile([P, H], F32, name="acc_%s_%d" % (side, j))
+                acc[side, j] = sums.tile([P, H], F32, name="acc_%s_%d" % (side, j))
 
         pair_bank = {}
-        last_bank = {}
+        small_bank = {}
         eq_t = {}
         squares = {}
+        partial = {}
         norm = {}
+        rsqrt = {}
         recip = {}
         xn = {}
-        codes = {}
-        planes = {}
+        xn_codes = {}
+        xn_planes = {}
 
-        def turn_in(s):
-            pair_bank[s] = banks.tile([P, 2, 2, P], F32, name="pair_bank")
-            last_bank[s] = banks.tile([P, 2, P], F32, name="last_bank")
+        def transpose_step(s):
+            pair_bank[s] = banks.tile([P, 2, 2, P], F32, name="pair_bank", tag="pair")
+            small_bank[s] = banks.tile([P, 2, P], F32, name="small_bank", tag="small")
             first, column = eq_home[s]
             for j in range(COMPONENTS):
                 words = eq_tiles[first][:, j, column : column + K_PASS].bitcast(F32)
-                transpose_pass(nc, pair_bank[s][:, j] if j < 2 else last_bank[s][:], words, identity)
+                transpose_pass(nc, pair_bank[s][:, j] if j < 2 else small_bank[s][:], words, identity)
 
-        def turn_out(s):
+        def copy_out(s):
             eq_t[s] = turned.tile([P, COMPONENTS, P, PACK], BF16, align_bytes=64, name="eq_t")
-            copy = nc.vector.tensor_copy if s < VECTOR_COPIES else nc.scalar.copy
-            copy(out=eq_t[s][:, 0:2].bitcast(F32), in_=pair_bank[s][:].rearrange("p j u b -> p j b u"))
-            copy(out=eq_t[s][:, 2].bitcast(F32), in_=last_bank[s][:].rearrange("p u b -> p b u"))
+            copy_pair = nc.vector.tensor_copy if s < FILL_STEPS else nc.scalar.copy
+            copy_small = nc.vector.tensor_copy if s < FILL_STEPS or s % 2 == 0 else nc.scalar.copy
+            copy_pair(out=eq_t[s][:, 0:2].bitcast(F32), in_=pair_bank[s][:].rearrange("p j u b -> p j b u"))
+            copy_small(out=eq_t[s][:, 2].bitcast(F32), in_=small_bank[s][:].rearrange("p u b -> p b u"))
 
         def square(s):
             squares[s] = work.tile([P, COMPONENTS, K_PASS], F32, name="squares")
             nc.scalar.activation(out=squares[s][:], in_=eq_t[s][:].rearrange("p j b t -> p j (b t)"), func=ACT.Square)
 
         def add_two(s):
-            norm[s] = work.tile([P, K_PASS], F32, name="norm")
+            partial[s] = work.tile([P, K_PASS], F32, name="partial")
             nc.vector.scalar_tensor_tensor(
-                out=norm[s][:], in0=squares[s][:, 0, :], scalar=EPSILON, in1=squares[s][:, 1, :], op0=ALU.add, op1=ALU.add
+                out=partial[s][:],
+                in0=squares[s][:, 0, :],
+                scalar=EPSILON,
+                in1=squares[s][:, 1, :],
+                op0=ALU.add,
+                op1=ALU.add,
             )
 
         def add_third(s):
-            nc.vector.tensor_tensor(out=norm[s][:], in0=norm[s][:], in1=squares[s][:, 2, :], op=ALU.add)
+            norm[s] = work.tile([P, K_PASS], F32, name="norm")
+            nc.vector.tensor_tensor(out=norm[s][:], in0=partial[s][:], in1=squares[s][:, 2, :], op=ALU.add)
 
         def root(s):
-            recip[s] = work.tile([P, K_PASS], F32, name="recip")
-            nc.scalar.activation(out=recip[s][:], in_=norm[s][:], func=ACT.Abs_reciprocal_sqrt)
+            rsqrt[s] = work.tile([P, K_PASS], F32, name="rsqrt")
+            nc.scalar.activation(out=rsqrt[s][:], in_=norm[s][:], func=ACT.Abs_reciprocal_sqrt)
 
         def root_squared(s):
-            nc.scalar.activation(out=recip[s][:], in_=recip[s][:], func=ACT.Square)
+            recip[s] = work.tile([P, K_PASS], F32, name="recip")
+            nc.scalar.activation(out=recip[s][:], in_=rsqrt[s][:], func=ACT.Square)
 
-        def scale(s):
+        def divide(s):
             xn[s] = work.tile([P, COMPONENTS, K_PASS], BF16, align_bytes=64, name="xn")
             nc.vector.tensor_tensor(
                 out=xn[s][:],
@@ -191,51 +206,55 @@ def tile_ryeelman_pa_k_kernel(
             )
 
         def quantise(s):
-            codes[s] = packed.tile([P, COMPONENTS, P], U32, align_bytes=64, name="codes")
-            planes[s] = packed.tile([P, COMPONENTS, P], U8, align_bytes=64, name="planes")
+            xn_codes[s] = packed.tile([P, COMPONENTS, P], U32, align_bytes=64, name="xn_codes")
+            xn_planes[s] = packed.tile([P, COMPONENTS, P], U8, align_bytes=64, name="xn_planes")
             for j in range(COMPONENTS):
-                nc.vector.quantize_mx(out=codes[s][:, j, :].bitcast(FP8X4), scales=planes[s][:, j, :], in_=xn[s][:, j, :])
+                nc.vector.quantize_mx(
+                    out=xn_codes[s][:, j, :].bitcast(FP8X4), scales=xn_planes[s][:, j, :], in_=xn[s][:, j, :]
+                )
 
         def contract(s):
             for j in range(COMPONENTS):
                 for side in SIDES:
                     nc.tensor.matmul_mx(
                         out=acc[side, j][:],
-                        lhsT=codes[s][:, j, :].bitcast(FP8X4),
-                        lhsT_scale=planes[s][:, j, :],
+                        lhsT=xn_codes[s][:, j, :].bitcast(FP8X4),
+                        lhsT_scale=xn_planes[s][:, j, :],
                         rhs=w_words[side][:, s, :].bitcast(FP8X4),
                         rhs_scale=w_planes[side][4 * (s % SHARE) : P, s // SHARE, :],
                         start=(s == 0),
                         stop=(s == STEPS - 1),
                     )
 
+        def is_step(s):
+            return 0 <= s < STEPS
+
         def period(s):
-            if 0 <= s + 2 < STEPS:
-                square(s + 2)
-            if 0 <= s + 1 < STEPS:
-                root(s + 1)
-            if 0 <= s + 3 < STEPS:
-                turn_out(s + 3)
-            if s + 4 < STEPS:
-                turn_in(s + 4)
-            if 0 <= s + 1 < STEPS:
-                root_squared(s + 1)
-            if 0 <= s:
-                scale(s)
-            if 0 <= s + 2 < STEPS:
-                add_two(s + 2)
-            if 0 <= s:
+            if is_step(s + SQUARE_AHEAD):
+                square(s + SQUARE_AHEAD)
+            if is_step(s + ROOT_AHEAD):
+                root(s + ROOT_AHEAD)
+            if is_step(s + COPY_AHEAD):
+                copy_out(s + COPY_AHEAD)
+            if is_step(s + TRANSPOSE_AHEAD):
+                transpose_step(s + TRANSPOSE_AHEAD)
+            if is_step(s + ROOT_AHEAD):
+                root_squared(s + ROOT_AHEAD)
+            if is_step(s):
+                divide(s)
+            if is_step(s + SQUARE_AHEAD):
+                add_two(s + SQUARE_AHEAD)
+            if is_step(s):
                 quantise(s)
-            if 0 <= s + 2 < STEPS:
-                add_third(s + 2)
-            if 0 <= s:
+            if is_step(s + SQUARE_AHEAD):
+                add_third(s + SQUARE_AHEAD)
+            if is_step(s):
                 contract(s)
 
-        turn_in(0)
-        for s in range(-3, STEPS - 3):
+        for s in range(-TRANSPOSE_AHEAD, STEPS - COPY_AHEAD):
             period(s)
 
-        inv_bank = banks.tile([P, II_PASSES, 2, P], F32, name="pair_bank")
+        inv_bank = banks.tile([P, II_PASSES, 2, P], F32, name="inv_bank", tag="pair")
         for c in range(II_PASSES):
             transpose_pass(nc, inv_bank[:, c], inv[:, K_PASS * c : K_PASS * (c + 1)].bitcast(F32), identity)
         inv_t = keep.tile([P, II_PASSES, P, PACK], BF16, align_bytes=64)
@@ -247,7 +266,7 @@ def tile_ryeelman_pa_k_kernel(
             scales=inv_planes[:].rearrange("p c b -> p (c b)"),
             in_=inv_t[:].rearrange("p c b t -> p (c b t)"),
         )
-        lin = banks.tile([P, H], F32, name="last_bank")
+        lin = banks.tile([P, H], F32, name="lin", tag="small")
         for c in range(II_PASSES):
             nc.tensor.matmul_mx(
                 out=lin[:],
@@ -259,7 +278,7 @@ def tile_ryeelman_pa_k_kernel(
                 stop=(c == II_PASSES - 1),
             )
 
-        for s in range(STEPS - 3, STEPS):
+        for s in range(STEPS - COPY_AHEAD, STEPS):
             period(s)
 
         nc.scalar.activation(out=warm[:, 1:2], in_=one[:], func=ACT.Tanh)

@@ -26,19 +26,12 @@ II_PASSES = FEATURES // K_PASS
 SIDES = ("left", "right")
 BLOCK = 16
 SHARE = 4
-EQ_LOADS = ((0, 1), (1, 1)) + tuple((first, 2) for first in range(2, STEPS, 2))
-TRANSPOSE_AHEAD = 4
-COPY_AHEAD = 3
-SQUARE_AHEAD = 2
-ROOT_AHEAD = 1
-FILL_STEPS = COPY_AHEAD + 1
+EQ_LOADS = ((1, 1), (0, 1), (2, 1), (3, 1)) + tuple((first, 2) for first in range(4, STEPS, 2))
+ORDER = tuple(first + i for first, count in EQ_LOADS for i in range(count))
+SWEEP_A = 7
+SWEEP_B = 4
 
 FLOPS = 2 * P * COMPONENTS * CHANNELS * H * 2 + 2 * P * FEATURES * H
-
-
-def transpose_pass(nc, halves, words, identity):
-    for u in range(2):
-        nc.tensor.transpose(halves[:, u, :], words[:, u:PASS_WORDS:2], identity[:])
 
 
 def load_words(nc, words_tile, words, first, count):
@@ -75,26 +68,18 @@ def tile_ryeelman_pa_k_kernel(
     with ExitStack() as stack:
         stack.enter_context(tc.manual_schedule())
         keep = stack.enter_context(tc.tile_pool(name="keep", bufs=1))
-        turned = stack.enter_context(tc.tile_pool(name="turned", bufs=COPY_AHEAD + 1))
         work = stack.enter_context(tc.tile_pool(name="work", bufs=2))
-        packed = stack.enter_context(tc.tile_pool(name="packed", bufs=3))
         sums = stack.enter_context(tc.psum_pool(name="sums", bufs=1))
         banks = stack.enter_context(tc.psum_pool(name="banks", bufs=1))
-
-        identity = keep.tile([P, P], F32)
-        make_identity(nc, identity[:])
 
         one = keep.tile([P, 1], F32)
         nc.vector.memset(one[:], 1.0)
         warm = keep.tile([P, 2], F32)
         nc.scalar.activation(out=warm[:, 0:1], in_=one[:], func=ACT.Abs_reciprocal_sqrt)
 
-        eq_tiles = {}
-        eq_home = {}
-        for first, count in EQ_LOADS:
-            eq_tiles[first] = keep.tile([P, COMPONENTS, count * K_PASS], BF16, align_bytes=64, name="eq_%d" % first)
-            for i in range(count):
-                eq_home[first + i] = (first, K_PASS * i)
+        identity = keep.tile([P, P], F32)
+        make_identity(nc, identity[:])
+
         first_input = keep.tile([P, COMPONENTS], BF16)
         first_hidden = keep.tile([P, COMPONENTS, BLOCK - 1], BF16)
         inv = keep.tile([P, FEATURES], BF16, align_bytes=64)
@@ -109,154 +94,194 @@ def tile_ryeelman_pa_k_kernel(
         for plane_tile in (w_planes["left"], w_planes["right"], ii_planes):
             nc.vector.memset(plane_tile[:].bitcast(I32), 0)
 
-        def load_eq(first, skip):
-            lo = K_PASS * first
-            hi = lo + eq_tiles[first].shape[2]
-            nc.sync.dma_start(out=eq_tiles[first][:, :, skip:], in_=equivariant_hidden[:, :, lo + skip - 1 : hi - 1])
+        eq = {}
 
-        nc.sync.dma_start(out=first_input[:], in_=equivariant_input)
-        nc.sync.dma_start(out=first_hidden[:], in_=equivariant_hidden[:, :, 0 : BLOCK - 1])
-        load_eq(0, BLOCK)
-        load_eq(1, 0)
-        load_eq(2, 0)
-        load_eq(4, 0)
-        for first in range(0, STEPS, 2):
-            if first % SHARE == 0:
-                load_scales(nc, w_planes["left"][:, first // SHARE, :], W_left_scales[first : first + SHARE])
-                load_scales(nc, w_planes["right"][:, first // SHARE, :], W_right_scales[first : first + SHARE])
-            load_words(nc, w_words["left"], W_left_words, first, 2)
-            load_words(nc, w_words["right"], W_right_words, first, 2)
-            if first + 6 < STEPS:
-                load_eq(first + 6, 0)
+        def load_eq(first, count):
+            tile = keep.tile([P, COMPONENTS, count * K_PASS], BF16, align_bytes=64, name="eq_%d" % first)
+            for i in range(count):
+                eq[first + i] = tile[:, :, K_PASS * i : K_PASS * (i + 1)]
+            lo = K_PASS * first
+            hi = lo + count * K_PASS
+            skip = BLOCK if first == 0 else 0
+            if first == ORDER[0]:
+                for j in range(COMPONENTS):
+                    nc.sync.dma_start(out=tile[:, j, :], in_=equivariant_hidden[:, j, lo - 1 : hi - 1])
+            else:
+                nc.sync.dma_start(out=tile[:, :, skip:], in_=equivariant_hidden[:, :, lo + skip - 1 : hi - 1])
+            if first == 0:
+                nc.sync.dma_start(out=first_input[:], in_=equivariant_input)
+                nc.sync.dma_start(out=first_hidden[:], in_=equivariant_hidden[:, :, 0 : BLOCK - 1])
+
+        def load_weights(first, count):
+            for side, words in zip(SIDES, (W_left_words, W_right_words)):
+                load_words(nc, w_words[side], words, first, count)
+
+        def load_weight_scales(g):
+            for side, scales in zip(SIDES, (W_left_scales, W_right_scales)):
+                load_scales(nc, w_planes[side][:, g, :], scales[SHARE * g : SHARE * (g + 1)])
+
+        for first, count in EQ_LOADS[:4]:
+            load_eq(first, count)
+        for i, (first, count) in enumerate(EQ_LOADS):
+            if i in (0, 4, 6, 8):
+                load_weight_scales(first // SHARE)
+            load_weights(first, count)
+            if 1 <= i and i + 3 < len(EQ_LOADS):
+                load_eq(EQ_LOADS[i + 3][0], EQ_LOADS[i + 3][1])
         nc.sync.dma_start(out=inv[:, 0 : FEATURES // 2], in_=invariant_input)
         nc.sync.dma_start(out=inv[:, FEATURES // 2 : FEATURES], in_=invariant_hidden)
-        load_words(nc, ii_words, W_ii_words, 0, II_PASSES)
         load_scales(nc, ii_planes[:], W_ii_scales)
+        load_words(nc, ii_words, W_ii_words, 0, II_PASSES)
         nc.sync.dma_start(out=bias[:], in_=b_ii.partition_broadcast(P))
-
-        nc.vector.tensor_copy(out=eq_tiles[0][:, :, 0:1], in_=first_input[:].unsqueeze(2))
-        nc.vector.tensor_copy(out=eq_tiles[0][:, :, 1:BLOCK], in_=first_hidden[:])
 
         acc = {}
         for side in SIDES:
             for j in range(COMPONENTS):
-                acc[side, j] = sums.tile([P, H], F32, name="acc_%s_%d" % (side, j))
+                if (side, j) != ("right", 2):
+                    acc[side, j] = sums.tile([P, H], F32, name="acc_%s_%d" % (side, j))
 
-        pair_bank = {}
-        small_bank = {}
-        eq_t = {}
         squares = {}
         partial = {}
         norm = {}
+        norm_bank = {}
         rsqrt = {}
         recip = {}
+        pair_bank = {}
+        small_bank = {}
         xn = {}
         xn_codes = {}
         xn_planes = {}
 
-        def transpose_step(s):
-            pair_bank[s] = banks.tile([P, 2, 2, P], F32, name="pair_bank", tag="pair")
-            small_bank[s] = banks.tile([P, 2, P], F32, name="small_bank", tag="small")
-            first, column = eq_home[s]
+        def square(i):
+            x = eq[ORDER[i]]
+            squares[i] = work.tile([P, COMPONENTS, K_PASS], F32, name="squares", bufs=3)
+            if ORDER[i] == 0:
+                nc.vector.tensor_copy(out=x[:, :, 0:1], in_=first_input[:].unsqueeze(2))
+                nc.vector.tensor_copy(out=x[:, :, 1:BLOCK], in_=first_hidden[:])
             for j in range(COMPONENTS):
-                words = eq_tiles[first][:, j, column : column + K_PASS].bitcast(F32)
-                transpose_pass(nc, pair_bank[s][:, j] if j < 2 else small_bank[s][:], words, identity)
+                if i == 0 and j == 2:
+                    nc.vector.tensor_tensor(out=squares[i][:, j, :], in0=x[:, j, :], in1=x[:, j, :], op=ALU.mult)
+                else:
+                    nc.scalar.activation(out=squares[i][:, j, :], in_=x[:, j, :], func=ACT.Square)
 
-        def copy_out(s):
-            eq_t[s] = turned.tile([P, COMPONENTS, P, PACK], BF16, align_bytes=64, name="eq_t")
-            copy_pair = nc.vector.tensor_copy if s < FILL_STEPS else nc.scalar.copy
-            copy_small = nc.vector.tensor_copy if s < FILL_STEPS or s % 2 == 0 else nc.scalar.copy
-            copy_pair(out=eq_t[s][:, 0:2].bitcast(F32), in_=pair_bank[s][:].rearrange("p j u b -> p j b u"))
-            copy_small(out=eq_t[s][:, 2].bitcast(F32), in_=small_bank[s][:].rearrange("p u b -> p b u"))
+        def add_two(i):
+            partial[i] = work.tile([P, K_PASS], F32, name="partial")
+            engine = nc.vector if i == 0 else nc.gpsimd
+            engine.tensor_tensor(out=partial[i][:], in0=squares[i][:, 0, :], in1=squares[i][:, 1, :], op=ALU.add)
 
-        def square(s):
-            squares[s] = work.tile([P, COMPONENTS, K_PASS], F32, name="squares")
-            nc.scalar.activation(out=squares[s][:], in_=eq_t[s][:].rearrange("p j b t -> p j (b t)"), func=ACT.Square)
-
-        def add_two(s):
-            partial[s] = work.tile([P, K_PASS], F32, name="partial")
+        def add_third(i):
+            norm[i] = work.tile([P, K_PASS], F32, name="norm")
             nc.vector.scalar_tensor_tensor(
-                out=partial[s][:],
-                in0=squares[s][:, 0, :],
+                out=norm[i][:],
+                in0=partial[i][:],
                 scalar=EPSILON,
-                in1=squares[s][:, 1, :],
+                in1=squares[i][:, 2, :],
                 op0=ALU.add,
                 op1=ALU.add,
             )
 
-        def add_third(s):
-            norm[s] = work.tile([P, K_PASS], F32, name="norm")
-            nc.vector.tensor_tensor(out=norm[s][:], in0=partial[s][:], in1=squares[s][:, 2, :], op=ALU.add)
+        def transpose_norm(i):
+            norm_bank[i] = banks.tile([P, PACK, P], F32, name="norm_bank", tag="norm")
+            for t in range(PACK):
+                nc.tensor.transpose(norm_bank[i][:, t, :], norm[i][:, t:K_PASS:PACK], identity[:])
 
-        def root(s):
-            rsqrt[s] = work.tile([P, K_PASS], F32, name="rsqrt")
-            nc.scalar.activation(out=rsqrt[s][:], in_=norm[s][:], func=ACT.Abs_reciprocal_sqrt)
+        def root(i):
+            rsqrt[i] = work.tile([P, P, PACK], F32, name="rsqrt")
+            nc.scalar.activation(
+                out=rsqrt[i][:], in_=norm_bank[i][:].rearrange("p t b -> p b t"), func=ACT.Abs_reciprocal_sqrt
+            )
 
-        def root_squared(s):
-            recip[s] = work.tile([P, K_PASS], F32, name="recip")
-            nc.scalar.activation(out=recip[s][:], in_=rsqrt[s][:], func=ACT.Square)
+        def root_squared(i):
+            recip[i] = work.tile([P, P, PACK], F32, name="recip")
+            nc.scalar.activation(out=recip[i][:], in_=rsqrt[i][:], func=ACT.Square)
 
-        def divide(s):
-            xn[s] = work.tile([P, COMPONENTS, K_PASS], BF16, align_bytes=64, name="xn")
+        def transpose_words(half_banks, words):
+            for u in range(2):
+                nc.tensor.transpose(half_banks[:, u, :], words[:, u:PASS_WORDS:2], identity[:])
+
+        def transpose_pair(i):
+            pair_bank[i] = banks.tile([P, 2, 2, P], F32, name="pair_bank", tag="pair")
+            for j in range(2):
+                transpose_words(pair_bank[i][:, j], eq[ORDER[i]][:, j, :].bitcast(F32))
+
+        def transpose_small(i):
+            small_bank[i] = banks.tile([P, 2, 2, P], F32, name="small_bank", tag="small")
+            transpose_words(small_bank[i][:, 0], eq[ORDER[i]][:, 2, :].bitcast(F32))
+
+        def divide(i, j):
+            if j == 0:
+                xn[i] = work.tile([P, COMPONENTS, P, PACK], BF16, align_bytes=64, name="xn")
+            bank = pair_bank[i][:, j] if j < 2 else small_bank[i][:, 0]
             nc.vector.tensor_tensor(
-                out=xn[s][:],
-                in0=eq_t[s][:].rearrange("p j b t -> p j (b t)"),
-                in1=recip[s][:].unsqueeze(1).to_broadcast([P, COMPONENTS, K_PASS]),
+                out=xn[i][:, j].rearrange("p b (u e) -> p b u e", u=2),
+                in0=bank.rearrange("p u b -> p (u b)").bitcast(BF16).rearrange("p (u b e) -> p b u e", u=2, e=2),
+                in1=recip[i][:].rearrange("p b (u e) -> p b u e", u=2),
                 op=ALU.mult,
             )
 
-        def quantise(s):
-            xn_codes[s] = packed.tile([P, COMPONENTS, P], U32, align_bytes=64, name="xn_codes")
-            xn_planes[s] = packed.tile([P, COMPONENTS, P], U8, align_bytes=64, name="xn_planes")
-            for j in range(COMPONENTS):
+        def quantise(i):
+            xn_codes[i] = keep.tile([P, COMPONENTS, P], U32, align_bytes=64, name="xn_codes_%d" % i)
+            xn_planes[i] = keep.tile([P, COMPONENTS, P], U8, align_bytes=64, name="xn_planes_%d" % i)
+            for js in (slice(0, 2), slice(2, 3)):
                 nc.vector.quantize_mx(
-                    out=xn_codes[s][:, j, :].bitcast(FP8X4), scales=xn_planes[s][:, j, :], in_=xn[s][:, j, :]
+                    out=xn_codes[i][:, js].rearrange("p j b -> p (j b)").bitcast(FP8X4),
+                    scales=xn_planes[i][:, js].rearrange("p j b -> p (j b)"),
+                    in_=xn[i][:, js].rearrange("p j b t -> p (j b t)"),
                 )
 
-        def contract(s):
-            for j in range(COMPONENTS):
-                for side in SIDES:
-                    nc.tensor.matmul_mx(
-                        out=acc[side, j][:],
-                        lhsT=xn_codes[s][:, j, :].bitcast(FP8X4),
-                        lhsT_scale=xn_planes[s][:, j, :],
-                        rhs=w_words[side][:, s, :].bitcast(FP8X4),
-                        rhs_scale=w_planes[side][4 * (s % SHARE) : P, s // SHARE, :],
-                        start=(s == 0),
-                        stop=(s == STEPS - 1),
-                    )
+        def contract(i, side, j):
+            step = ORDER[i]
+            nc.tensor.matmul_mx(
+                out=acc[side, j][:],
+                lhsT=xn_codes[i][:, j, :].bitcast(FP8X4),
+                lhsT_scale=xn_planes[i][:, j, :],
+                rhs=w_words[side][:, step, :].bitcast(FP8X4),
+                rhs_scale=w_planes[side][4 * (step % SHARE) : P, step // SHARE, :],
+                start=(i == 0),
+                stop=(i == STEPS - 1),
+            )
 
-        def is_step(s):
-            return 0 <= s < STEPS
+        def contract_open(i):
+            for side, j in (("left", 0), ("right", 0), ("left", 1), ("right", 1), ("left", 2)):
+                contract(i, side, j)
 
-        def period(s):
-            if is_step(s + SQUARE_AHEAD):
-                square(s + SQUARE_AHEAD)
-            if is_step(s + ROOT_AHEAD):
-                root(s + ROOT_AHEAD)
-            if is_step(s + COPY_AHEAD):
-                copy_out(s + COPY_AHEAD)
-            if is_step(s + TRANSPOSE_AHEAD):
-                transpose_step(s + TRANSPOSE_AHEAD)
-            if is_step(s + ROOT_AHEAD):
-                root_squared(s + ROOT_AHEAD)
-            if is_step(s):
-                divide(s)
-            if is_step(s + SQUARE_AHEAD):
-                add_two(s + SQUARE_AHEAD)
-            if is_step(s):
-                quantise(s)
-            if is_step(s + SQUARE_AHEAD):
-                add_third(s + SQUARE_AHEAD)
-            if is_step(s):
-                contract(s)
+        def is_step(i):
+            return 0 <= i < STEPS
 
-        for s in range(-TRANSPOSE_AHEAD, STEPS - COPY_AHEAD):
-            period(s)
+        def front(i):
+            if is_step(i):
+                divide(i, 0)
+                divide(i, 1)
+            if is_step(i + 1):
+                transpose_norm(i + 1)
+                root(i + 1)
+                root_squared(i + 1)
+                transpose_pair(i + 1)
+            if is_step(i):
+                divide(i, 2)
+            if is_step(i + 1):
+                transpose_small(i + 1)
+            if is_step(i + 3):
+                square(i + 3)
+                add_two(i + 3)
+            if is_step(i):
+                quantise(i)
+            if is_step(i + 2):
+                add_third(i + 2)
 
+        for i in range(-3, STEPS - 1):
+            front(i)
+            if is_step(i):
+                contract_open(i)
+
+        acc["right", 2] = banks.tile([P, H], F32, name="acc_right_2", tag="norm")
+        nc.scalar.activation(out=warm[:, 1:2], in_=one[:], func=ACT.Tanh)
+        for i in range(SWEEP_A):
+            contract(i, "right", 2)
+        front(STEPS - 1)
         inv_bank = banks.tile([P, II_PASSES, 2, P], F32, name="inv_bank", tag="pair")
         for c in range(II_PASSES):
-            transpose_pass(nc, inv_bank[:, c], inv[:, K_PASS * c : K_PASS * (c + 1)].bitcast(F32), identity)
+            transpose_words(inv_bank[:, c], inv[:, K_PASS * c : K_PASS * (c + 1)].bitcast(F32))
         inv_t = keep.tile([P, II_PASSES, P, PACK], BF16, align_bytes=64)
         nc.scalar.copy(out=inv_t[:].bitcast(F32), in_=inv_bank[:].rearrange("p c u b -> p c b u"))
         inv_codes = keep.tile([P, II_PASSES, P], U32, align_bytes=64)
@@ -266,6 +291,8 @@ def tile_ryeelman_pa_k_kernel(
             scales=inv_planes[:].rearrange("p c b -> p (c b)"),
             in_=inv_t[:].rearrange("p c b t -> p (c b t)"),
         )
+        for i in range(SWEEP_A, SWEEP_A + SWEEP_B):
+            contract(i, "right", 2)
         lin = banks.tile([P, H], F32, name="lin", tag="small")
         for c in range(II_PASSES):
             nc.tensor.matmul_mx(
@@ -277,19 +304,29 @@ def tile_ryeelman_pa_k_kernel(
                 start=(c == 0),
                 stop=(c == II_PASSES - 1),
             )
+        contract_open(STEPS - 1)
+        for i in range(SWEEP_A + SWEEP_B, STEPS):
+            contract(i, "right", 2)
 
-        for s in range(STEPS - COPY_AHEAD, STEPS):
-            period(s)
-
-        nc.scalar.activation(out=warm[:, 1:2], in_=one[:], func=ACT.Tanh)
-        total = keep.tile([P, H], F32)
-        nc.vector.tensor_tensor(out=total[:], in0=lin[:], in1=bias[:], op=ALU.add)
+        lin_b = keep.tile([P, H], F32)
+        nc.vector.tensor_tensor(out=lin_b[:], in0=lin[:], in1=bias[:], op=ALU.add)
+        left = []
+        product = []
         for j in range(COMPONENTS):
-            left = keep.tile([P, H], F32, name="left_%d" % j)
-            nc.scalar.copy(out=left[:], in_=acc["left", j][:])
-            product = keep.tile([P, H], F32, name="product_%d" % j)
-            nc.vector.tensor_tensor(out=product[:], in0=left[:], in1=acc["right", j][:], op=ALU.mult)
-            nc.vector.tensor_tensor(out=total[:], in0=total[:], in1=product[:], op=ALU.add)
+            left.append(keep.tile([P, H], F32, name="left_%d" % j))
+            nc.scalar.copy(out=left[j][:], in_=acc["left", j][:])
+            product.append(keep.tile([P, H], F32, name="product_%d" % j))
+        for j in range(2):
+            nc.vector.tensor_tensor(out=product[j][:], in0=left[j][:], in1=acc["right", j][:], op=ALU.mult)
+        partial_sum = keep.tile([P, H], F32)
+        total = keep.tile([P, H], F32)
         result = keep.tile([P, H], F32)
-        nc.scalar.activation(out=result[:], in_=total[:], func=ACT.Tanh)
-        nc.sync.dma_start(out=out, in_=result[:])
+        nc.vector.tensor_tensor(out=partial_sum[:], in0=lin_b[:], in1=product[0][:], op=ALU.add)
+        nc.vector.tensor_tensor(out=total[:], in0=partial_sum[:], in1=product[1][:], op=ALU.add)
+        halves = (slice(0, H // 2), slice(H // 2, H))
+        for cols in halves:
+            nc.vector.tensor_tensor(out=product[2][:, cols], in0=left[2][:, cols], in1=acc["right", 2][:, cols], op=ALU.mult)
+        for cols in halves:
+            nc.vector.tensor_tensor(out=partial_sum[:, cols], in0=total[:, cols], in1=product[2][:, cols], op=ALU.add)
+            nc.scalar.activation(out=result[:, cols], in_=partial_sum[:, cols], func=ACT.Tanh)
+            nc.sync.dma_start(out=out[:, cols], in_=result[:, cols])

@@ -165,7 +165,7 @@ def tile_ryeelman_pa_k_kernel(
                     nc.scalar.activation(out=squares[i][:, j, :], in_=x[:, j, :], func=ACT.Square)
 
         def add_two(i):
-            partial[i] = work.tile([P, K_PASS], F32, name="partial")
+            partial[i] = work.tile([P, K_PASS], F32, name="partial", bufs=1)
             engine = nc.vector if i == 0 else nc.gpsimd
             engine.tensor_tensor(out=partial[i][:], in0=squares[i][:, 0, :], in1=squares[i][:, 1, :], op=ALU.add)
 
@@ -263,11 +263,12 @@ def tile_ryeelman_pa_k_kernel(
                 transpose_small(i + 1)
             if is_step(i + 3):
                 square(i + 3)
-                add_two(i + 3)
             if is_step(i):
                 quantise(i)
             if is_step(i + 2):
                 add_third(i + 2)
+            if is_step(i + 3):
+                add_two(i + 3)
 
         for i in range(-3, STEPS - 1):
             front(i)

@@ -159,10 +159,12 @@ def tile_ryeelman_pa_k_kernel(
                 nc.vector.tensor_copy(out=x[:, :, 0:1], in_=first_input[:].unsqueeze(2))
                 nc.vector.tensor_copy(out=x[:, :, 1:BLOCK], in_=first_hidden[:])
             for j in range(COMPONENTS):
+                sq = squares[i][:, j, :].rearrange("b (t p) -> b t p", t=PACK)
+                xj = x[:, j, :].rearrange("b (p t) -> b t p", t=PACK)
                 if i == 0 and j == 2:
-                    nc.vector.tensor_tensor(out=squares[i][:, j, :], in0=x[:, j, :], in1=x[:, j, :], op=ALU.mult)
+                    nc.vector.tensor_tensor(out=sq, in0=xj, in1=xj, op=ALU.mult)
                 else:
-                    nc.scalar.activation(out=squares[i][:, j, :], in_=x[:, j, :], func=ACT.Square)
+                    nc.scalar.activation(out=sq, in_=xj, func=ACT.Square)
 
         def add_two(i):
             partial[i] = work.tile([P, K_PASS], F32, name="partial", bufs=1)
@@ -183,7 +185,7 @@ def tile_ryeelman_pa_k_kernel(
         def transpose_norm(i):
             norm_bank[i] = banks.tile([P, PACK, P], F32, name="norm_bank", tag="norm")
             for t in range(PACK):
-                nc.tensor.transpose(norm_bank[i][:, t, :], norm[i][:, t:K_PASS:PACK], identity[:])
+                nc.tensor.transpose(norm_bank[i][:, t, :], norm[i][:, P * t : P * (t + 1)], identity[:])
 
         def root(i):
             rsqrt[i] = work.tile([P, P, PACK], F32, name="rsqrt")

@@ -152,19 +152,19 @@ def tile_ryeelman_pa_k_kernel(
         xn_codes = {}
         xn_planes = {}
 
-        def square(i):
+        def square(i, j):
             x = eq[ORDER[i]]
-            squares[i] = work.tile([P, COMPONENTS, K_PASS], F32, name="squares", bufs=3)
-            if ORDER[i] == 0:
-                nc.vector.tensor_copy(out=x[:, :, 0:1], in_=first_input[:].unsqueeze(2))
-                nc.vector.tensor_copy(out=x[:, :, 1:BLOCK], in_=first_hidden[:])
-            for j in range(COMPONENTS):
-                sq = squares[i][:, j, :].rearrange("b (t p) -> b t p", t=PACK)
-                xj = x[:, j, :].rearrange("b (p t) -> b t p", t=PACK)
-                if i == 0 and j == 2:
-                    nc.vector.tensor_tensor(out=sq, in0=xj, in1=xj, op=ALU.mult)
-                else:
-                    nc.scalar.activation(out=sq, in_=xj, func=ACT.Square)
+            if j == 0:
+                squares[i] = work.tile([P, COMPONENTS, K_PASS], F32, name="squares", bufs=3)
+                if ORDER[i] == 0:
+                    nc.vector.tensor_copy(out=x[:, :, 0:1], in_=first_input[:].unsqueeze(2))
+                    nc.vector.tensor_copy(out=x[:, :, 1:BLOCK], in_=first_hidden[:])
+            sq = squares[i][:, j, :].rearrange("b (t p) -> b t p", t=PACK)
+            xj = x[:, j, :].rearrange("b (p t) -> b t p", t=PACK)
+            if i == 0 and j == 2:
+                nc.vector.tensor_tensor(out=sq, in0=xj, in1=xj, op=ALU.mult)
+            else:
+                nc.scalar.activation(out=sq, in_=xj, func=ACT.Square)
 
         def add_two(i):
             partial[i] = work.tile([P, K_PASS], F32, name="partial", bufs=1)
@@ -194,7 +194,7 @@ def tile_ryeelman_pa_k_kernel(
             )
 
         def root_squared(i):
-            recip[i] = work.tile([P, P, PACK], F32, name="recip")
+            recip[i] = work.tile([P, P, PACK], F32, name="recip", bufs=3)
             nc.scalar.activation(out=recip[i][:], in_=rsqrt[i][:], func=ACT.Square)
 
         def transpose_words(half_banks, words):
@@ -253,26 +253,34 @@ def tile_ryeelman_pa_k_kernel(
         def front(i):
             if is_step(i):
                 divide(i, 0)
+            if is_step(i + 2):
+                add_third(i + 2)
+            if is_step(i + 3):
+                add_two(i + 3)
+            if is_step(i + 2):
+                transpose_norm(i + 2)
+                root(i + 2)
+                if i < 0:
+                    root_squared(i + 2)
+            if is_step(i + 4):
+                square(i + 4, 0)
+                square(i + 4, 1)
+            if is_step(i + 2) and i >= 0:
+                root_squared(i + 2)
+            if is_step(i + 4):
+                square(i + 4, 2)
+            if is_step(i):
                 divide(i, 1)
             if is_step(i + 1):
-                transpose_norm(i + 1)
-                root(i + 1)
-                root_squared(i + 1)
                 transpose_pair(i + 1)
             if is_step(i):
                 divide(i, 2)
             if is_step(i + 1):
                 transpose_small(i + 1)
-            if is_step(i + 3):
-                square(i + 3)
             if is_step(i):
                 quantise(i)
-            if is_step(i + 2):
-                add_third(i + 2)
-            if is_step(i + 3):
-                add_two(i + 3)
 
-        for i in range(-3, STEPS - 1):
+        for i in range(-4, STEPS - 1):
             front(i)
             if is_step(i):
                 contract_open(i)

@@ -28,6 +28,7 @@ BLOCK = 16
 SHARE = 4
 EQ_LOADS = ((1, 1), (0, 1), (2, 1), (3, 1)) + tuple((first, 2) for first in range(4, STEPS, 2))
 ORDER = tuple(first + i for first, count in EQ_LOADS for i in range(count))
+FILLING = 1
 SWEEP_A = 7
 SWEEP_B = 4
 
@@ -250,15 +251,14 @@ def tile_ryeelman_pa_k_kernel(
         def is_step(i):
             return 0 <= i < STEPS
 
-        def front(i):
-            if is_step(i):
-                divide(i, 0)
+        def sum_up(i):
             if is_step(i + 2):
                 add_third(i + 2)
             if is_step(i + 3):
                 add_two(i + 3)
+
+        def invert(i):
             if is_step(i + 2):
-                transpose_norm(i + 2)
                 root(i + 2)
                 if i < 0:
                     root_squared(i + 2)
@@ -269,16 +269,31 @@ def tile_ryeelman_pa_k_kernel(
                 root_squared(i + 2)
             if is_step(i + 4):
                 square(i + 4, 2)
+
+        def front(i):
+            filling = i <= FILLING
+            if i == -1:
+                transpose_pair(0)
+                transpose_small(0)
+            if not filling:
+                sum_up(i)
+                if is_step(i + 2):
+                    transpose_norm(i + 2)
+                invert(i)
             if is_step(i):
+                divide(i, 0)
                 divide(i, 1)
-            if is_step(i + 1):
-                transpose_pair(i + 1)
-            if is_step(i):
+                if is_step(i + 1):
+                    transpose_pair(i + 1)
                 divide(i, 2)
-            if is_step(i + 1):
-                transpose_small(i + 1)
-            if is_step(i):
+                if is_step(i + 1):
+                    transpose_small(i + 1)
                 quantise(i)
+            if filling:
+                sum_up(i)
+                if is_step(i + 2):
+                    transpose_norm(i + 2)
+                invert(i)
 
         for i in range(-4, STEPS - 1):
             front(i)

@@ -123,12 +123,12 @@ def tile_ryeelman_pa_k_kernel(
 
         for first, count in EQ_LOADS[:4]:
             load_eq(first, count)
-        for i, (first, count) in enumerate(EQ_LOADS):
-            if i in (0, 4, 6, 8):
-                load_weight_scales(first // SHARE)
-            load_weights(first, count)
-            if 1 <= i and i + 3 < len(EQ_LOADS):
-                load_eq(EQ_LOADS[i + 3][0], EQ_LOADS[i + 3][1])
+        for i, step in enumerate(ORDER):
+            if i % SHARE == 0:
+                load_weight_scales(i // SHARE)
+            load_weights(step, 1)
+            if i % 2 == 0 and i // 2 + 4 < len(EQ_LOADS):
+                load_eq(EQ_LOADS[i // 2 + 4][0], EQ_LOADS[i // 2 + 4][1])
         nc.sync.dma_start(out=inv[:, 0 : FEATURES // 2], in_=invariant_input)
         nc.sync.dma_start(out=inv[:, FEATURES // 2 : FEATURES], in_=invariant_hidden)
         load_scales(nc, ii_planes[:], W_ii_scales)

@@ -277,8 +277,15 @@ def tile_ryeelman_pa_k_kernel(
                 transpose_small(0)
             if not filling:
                 sum_up(i)
+                if FILLING + 1 < i < STEPS - 1:
+                    contract(i - 1, "left", 0)
+                    contract(i - 1, "right", 0)
                 if is_step(i + 2):
                     transpose_norm(i + 2)
+                if FILLING + 1 < i < STEPS - 1:
+                    contract(i - 1, "left", 1)
+                    contract(i - 1, "right", 1)
+                    contract(i - 1, "left", 2)
                 invert(i)
             if is_step(i):
                 divide(i, 0)
@@ -297,8 +304,9 @@ def tile_ryeelman_pa_k_kernel(
 
         for i in range(-4, STEPS - 1):
             front(i)
-            if is_step(i):
+            if 0 <= i <= FILLING:
                 contract_open(i)
+        contract_open(STEPS - 2)
 
         acc["right", 2] = banks.tile([P, H], F32, name="acc_right_2", tag="norm")
         nc.scalar.activation(out=warm[:, 1:2], in_=one[:], func=ACT.Tanh)

@@ -26,11 +26,10 @@ II_PASSES = FEATURES // K_PASS
 SIDES = ("left", "right")
 BLOCK = 16
 SHARE = 4
-EQ_LOADS = ((1, 1), (0, 1), (2, 1), (3, 1)) + tuple((first, 2) for first in range(4, STEPS, 2))
+EQ_LOADS = ((1, 1), (2, 1), (0, 1), (3, 1)) + tuple((first, 2) for first in range(4, STEPS, 2))
 ORDER = tuple(first + i for first, count in EQ_LOADS for i in range(count))
+SWEEP_AHEAD = 9
 FILLING = 1
-SWEEP_A = 7
-SWEEP_B = 4
 
 FLOPS = 2 * P * COMPONENTS * CHANNELS * H * 2 + 2 * P * FEATURES * H
 
@@ -121,7 +120,11 @@ def tile_ryeelman_pa_k_kernel(
             for side, scales in zip(SIDES, (W_left_scales, W_right_scales)):
                 load_scales(nc, w_planes[side][:, g, :], scales[SHARE * g : SHARE * (g + 1)])
 
-        for first, count in EQ_LOADS[:4]:
+        for first, count in EQ_LOADS[:2]:
+            load_eq(first, count)
+        nc.sync.dma_start(out=inv[:, 0 : FEATURES // 2], in_=invariant_input)
+        nc.sync.dma_start(out=inv[:, FEATURES // 2 : FEATURES], in_=invariant_hidden)
+        for first, count in EQ_LOADS[2:4]:
             load_eq(first, count)
         for i, step in enumerate(ORDER):
             if i % SHARE == 0:
@@ -129,8 +132,6 @@ def tile_ryeelman_pa_k_kernel(
             load_weights(step, 1)
             if i % 2 == 0 and i // 2 + 4 < len(EQ_LOADS):
                 load_eq(EQ_LOADS[i // 2 + 4][0], EQ_LOADS[i // 2 + 4][1])
-        nc.sync.dma_start(out=inv[:, 0 : FEATURES // 2], in_=invariant_input)
-        nc.sync.dma_start(out=inv[:, FEATURES // 2 : FEATURES], in_=invariant_hidden)
         load_scales(nc, ii_planes[:], W_ii_scales)
         load_words(nc, ii_words, W_ii_words, 0, II_PASSES)
         nc.sync.dma_start(out=bias[:], in_=b_ii.partition_broadcast(P))
@@ -248,8 +249,41 @@ def tile_ryeelman_pa_k_kernel(
             for side, j in (("left", 0), ("right", 0), ("left", 1), ("right", 1), ("left", 2)):
                 contract(i, side, j)
 
+        right_2 = []
+
+        def sweep(first, last, h):
+            for i in range(first, last):
+                step = ORDER[i]
+                cols = slice(h * H // 2, (h + 1) * H // 2)
+                nc.tensor.matmul_mx(
+                    out=right_2[h][:],
+                    lhsT=xn_codes[i][:, 2, :].bitcast(FP8X4),
+                    lhsT_scale=xn_planes[i][:, 2, :],
+                    rhs=w_words["right"][:, step, PACK * cols.start : PACK * cols.stop].bitcast(FP8X4),
+                    rhs_scale=w_planes["right"][4 * (step % SHARE) : P, step // SHARE, cols],
+                    start=(i == 0),
+                    stop=(i == STEPS - 1),
+                )
+
         def is_step(i):
             return 0 <= i < STEPS
+
+        inv_bank = acc["left", 0][:].rearrange("p (c u b) -> p c u b", c=II_PASSES, u=2)
+        inv_t = keep.tile([P, II_PASSES, P, PACK], BF16, align_bytes=64)
+        inv_codes = keep.tile([P, II_PASSES, P], U32, align_bytes=64)
+        inv_planes = keep.tile([P, II_PASSES, P], U8, align_bytes=64)
+
+        def transpose_inv():
+            for c in range(II_PASSES):
+                transpose_words(inv_bank[:, c], inv[:, K_PASS * c : K_PASS * (c + 1)].bitcast(F32))
+
+        def quantise_inv():
+            nc.vector.tensor_copy(out=inv_t[:].bitcast(F32), in_=inv_bank.rearrange("p c u b -> p c b u"))
+            nc.vector.quantize_mx(
+                out=inv_codes[:].rearrange("p c b -> p (c b)").bitcast(FP8X4),
+                scales=inv_planes[:].rearrange("p c b -> p (c b)"),
+                in_=inv_t[:].rearrange("p c b t -> p (c b t)"),
+            )
 
         def sum_up(i):
             if is_step(i + 2):
@@ -272,9 +306,10 @@ def tile_ryeelman_pa_k_kernel(
 
         def front(i):
             filling = i <= FILLING
-            if i == -1:
+            if i == -2:
                 transpose_pair(0)
                 transpose_small(0)
+                transpose_inv()
             if not filling:
                 sum_up(i)
                 if FILLING + 1 < i < STEPS - 1:
@@ -286,6 +321,8 @@ def tile_ryeelman_pa_k_kernel(
                     contract(i - 1, "left", 1)
                     contract(i - 1, "right", 1)
                     contract(i - 1, "left", 2)
+                if i == STEPS - 2:
+                    sweep(0, 2, 0)
                 invert(i)
             if is_step(i):
                 divide(i, 0)
@@ -295,6 +332,8 @@ def tile_ryeelman_pa_k_kernel(
                 divide(i, 2)
                 if is_step(i + 1):
                     transpose_small(i + 1)
+                if i == STEPS - 2:
+                    sweep(2, 4, 0)
                 quantise(i)
             if filling:
                 sum_up(i)
@@ -303,30 +342,19 @@ def tile_ryeelman_pa_k_kernel(
                 invert(i)
 
         for i in range(-4, STEPS - 1):
+            if i == STEPS - 2:
+                right_2.append(banks.tile([P, H // 2], F32, name="right_2_first", tag="norm"))
             front(i)
+            if i == -2:
+                quantise_inv()
             if 0 <= i <= FILLING:
                 contract_open(i)
         contract_open(STEPS - 2)
 
-        acc["right", 2] = banks.tile([P, H], F32, name="acc_right_2", tag="norm")
         nc.scalar.activation(out=warm[:, 1:2], in_=one[:], func=ACT.Tanh)
-        for i in range(SWEEP_A):
-            contract(i, "right", 2)
+        sweep(4, SWEEP_AHEAD, 0)
         front(STEPS - 1)
-        inv_bank = banks.tile([P, II_PASSES, 2, P], F32, name="inv_bank", tag="pair")
-        for c in range(II_PASSES):
-            transpose_words(inv_bank[:, c], inv[:, K_PASS * c : K_PASS * (c + 1)].bitcast(F32))
-        inv_t = keep.tile([P, II_PASSES, P, PACK], BF16, align_bytes=64)
-        nc.scalar.copy(out=inv_t[:].bitcast(F32), in_=inv_bank[:].rearrange("p c u b -> p c b u"))
-        inv_codes = keep.tile([P, II_PASSES, P], U32, align_bytes=64)
-        inv_planes = keep.tile([P, II_PASSES, P], U8, align_bytes=64)
-        nc.vector.quantize_mx(
-            out=inv_codes[:].rearrange("p c b -> p (c b)").bitcast(FP8X4),
-            scales=inv_planes[:].rearrange("p c b -> p (c b)"),
-            in_=inv_t[:].rearrange("p c b t -> p (c b t)"),
-        )
-        for i in range(SWEEP_A, SWEEP_A + SWEEP_B):
-            contract(i, "right", 2)
+        contract_open(STEPS - 1)
         lin = banks.tile([P, H], F32, name="lin", tag="small")
         for c in range(II_PASSES):
             nc.tensor.matmul_mx(
@@ -338,29 +366,41 @@ def tile_ryeelman_pa_k_kernel(
                 start=(c == 0),
                 stop=(c == II_PASSES - 1),
             )
-        contract_open(STEPS - 1)
-        for i in range(SWEEP_A + SWEEP_B, STEPS):
-            contract(i, "right", 2)
+        sweep(SWEEP_AHEAD, STEPS, 0)
+        right_2.append(banks.tile([P, H // 2], F32, name="right_2_second", tag="pair"))
+        sweep(0, STEPS, 1)
 
-        lin_b = keep.tile([P, H], F32)
-        nc.vector.tensor_tensor(out=lin_b[:], in0=lin[:], in1=bias[:], op=ALU.add)
         left = []
         product = []
         for j in range(COMPONENTS):
             left.append(keep.tile([P, H], F32, name="left_%d" % j))
             nc.scalar.copy(out=left[j][:], in_=acc["left", j][:])
             product.append(keep.tile([P, H], F32, name="product_%d" % j))
-        for j in range(2):
+        def multiply(j):
             nc.vector.tensor_tensor(out=product[j][:], in0=left[j][:], in1=acc["right", j][:], op=ALU.mult)
+
+        lin_b = keep.tile([P, H], F32)
         partial_sum = keep.tile([P, H], F32)
         total = keep.tile([P, H], F32)
+        final_sum = keep.tile([P, H], F32)
         result = keep.tile([P, H], F32)
-        nc.vector.tensor_tensor(out=partial_sum[:], in0=lin_b[:], in1=product[0][:], op=ALU.add)
-        nc.vector.tensor_tensor(out=total[:], in0=partial_sum[:], in1=product[1][:], op=ALU.add)
         halves = (slice(0, H // 2), slice(H // 2, H))
-        for cols in halves:
-            nc.vector.tensor_tensor(out=product[2][:, cols], in0=left[2][:, cols], in1=acc["right", 2][:, cols], op=ALU.mult)
-        for cols in halves:
-            nc.vector.tensor_tensor(out=partial_sum[:, cols], in0=total[:, cols], in1=product[2][:, cols], op=ALU.add)
-            nc.scalar.activation(out=result[:, cols], in_=partial_sum[:, cols], func=ACT.Tanh)
+
+        def multiply_half(h):
+            nc.vector.tensor_tensor(out=product[2][:, halves[h]], in0=left[2][:, halves[h]], in1=right_2[h][:], op=ALU.mult)
+
+        def finish_half(h):
+            cols = halves[h]
+            nc.vector.tensor_tensor(out=final_sum[:, cols], in0=total[:, cols], in1=product[2][:, cols], op=ALU.add)
+            nc.scalar.activation(out=result[:, cols], in_=final_sum[:, cols], func=ACT.Tanh)
             nc.sync.dma_start(out=out[:, cols], in_=result[:, cols])
+
+        multiply(0)
+        nc.vector.tensor_tensor(out=lin_b[:], in0=lin[:], in1=bias[:], op=ALU.add)
+        multiply(1)
+        nc.vector.tensor_tensor(out=partial_sum[:], in0=lin_b[:], in1=product[0][:], op=ALU.add)
+        multiply_half(0)
+        nc.vector.tensor_tensor(out=total[:], in0=partial_sum[:], in1=product[1][:], op=ALU.add)
+        finish_half(0)
+        multiply_half(1)
+        finish_half(1)

@@ -29,7 +29,7 @@ SHARE = 4
 EQ_LOADS = ((1, 1), (2, 1), (0, 1), (3, 1)) + tuple((first, 2) for first in range(4, STEPS, 2))
 ORDER = tuple(first + i for first, count in EQ_LOADS for i in range(count))
 SWEEP_AHEAD = 9
-FILLING = 1
+FILLING = -1
 
 FLOPS = 2 * P * COMPONENTS * CHANNELS * H * 2 + 2 * P * FEATURES * H
 
@@ -163,14 +163,14 @@ def tile_ryeelman_pa_k_kernel(
                     nc.vector.tensor_copy(out=x[:, :, 1:BLOCK], in_=first_hidden[:])
             sq = squares[i][:, j, :].rearrange("b (t p) -> b t p", t=PACK)
             xj = x[:, j, :].rearrange("b (p t) -> b t p", t=PACK)
-            if i == 0 and j == 2:
+            if i == 0 and j == 1:
                 nc.vector.tensor_tensor(out=sq, in0=xj, in1=xj, op=ALU.mult)
             else:
                 nc.scalar.activation(out=sq, in_=xj, func=ACT.Square)
 
         def add_two(i):
             partial[i] = work.tile([P, K_PASS], F32, name="partial", bufs=1)
-            engine = nc.vector if i == 0 else nc.gpsimd
+            engine = nc.vector if i in (0, 2) else nc.gpsimd
             engine.tensor_tensor(out=partial[i][:], in0=squares[i][:, 0, :], in1=squares[i][:, 1, :], op=ALU.add)
 
         def add_third(i):
@@ -277,8 +277,10 @@ def tile_ryeelman_pa_k_kernel(
             for c in range(II_PASSES):
                 transpose_words(inv_bank[:, c], inv[:, K_PASS * c : K_PASS * (c + 1)].bitcast(F32))
 
-        def quantise_inv():
+        def copy_inv():
             nc.vector.tensor_copy(out=inv_t[:].bitcast(F32), in_=inv_bank.rearrange("p c u b -> p c b u"))
+
+        def quantise_inv():
             nc.vector.quantize_mx(
                 out=inv_codes[:].rearrange("p c b -> p (c b)").bitcast(FP8X4),
                 scales=inv_planes[:].rearrange("p c b -> p (c b)"),
@@ -292,17 +294,15 @@ def tile_ryeelman_pa_k_kernel(
                 add_two(i + 3)
 
         def invert(i):
-            if is_step(i + 2):
-                root(i + 2)
-                if i < 0:
-                    root_squared(i + 2)
             if is_step(i + 4):
                 square(i + 4, 0)
                 square(i + 4, 1)
-            if is_step(i + 2) and i >= 0:
-                root_squared(i + 2)
+            if is_step(i + 2):
+                root(i + 2)
             if is_step(i + 4):
                 square(i + 4, 2)
+            if is_step(i + 2):
+                root_squared(i + 2)
 
         def front(i):
             filling = i <= FILLING
@@ -313,14 +313,9 @@ def tile_ryeelman_pa_k_kernel(
             if not filling:
                 sum_up(i)
                 if FILLING + 1 < i < STEPS - 1:
-                    contract(i - 1, "left", 0)
-                    contract(i - 1, "right", 0)
+                    contract_open(i - 1)
                 if is_step(i + 2):
                     transpose_norm(i + 2)
-                if FILLING + 1 < i < STEPS - 1:
-                    contract(i - 1, "left", 1)
-                    contract(i - 1, "right", 1)
-                    contract(i - 1, "left", 2)
                 if i == STEPS - 2:
                     sweep(0, 2, 0)
                 invert(i)
@@ -346,6 +341,7 @@ def tile_ryeelman_pa_k_kernel(
                 right_2.append(banks.tile([P, H // 2], F32, name="right_2_first", tag="norm"))
             front(i)
             if i == -2:
+                copy_inv()
                 quantise_inv()
             if 0 <= i <= FILLING:
                 contract_open(i)

from contextlib import ExitStack

import concourse.mybir as mybir
from concourse.masks import make_identity

F32 = mybir.dt.float32
BF16 = mybir.dt.bfloat16
I32 = mybir.dt.int32
U32 = mybir.dt.uint32
U8 = mybir.dt.uint8
FP8X4 = mybir.dt.float8_e4m3fn_x4
ACT = mybir.ActivationFunctionType
ALU = mybir.AluOpType

P = 128
PACK = 4
K_PASS = P * PACK
PASS_WORDS = K_PASS // 2
COMPONENTS = 3
CHANNELS = 8192
FEATURES = 1024
H = 512
EPSILON = 1e-6
STEPS = CHANNELS // K_PASS
II_PASSES = FEATURES // K_PASS
SIDES = ("left", "right")
BLOCK = 16
SHARE = 4
EQ_LOADS = ((1, 1), (2, 1), (0, 1), (3, 1)) + tuple((first, 2) for first in range(4, STEPS, 2))
ORDER = tuple(first + i for first, count in EQ_LOADS for i in range(count))
SWEEP_AHEAD = 9
FILLING = -1

FLOPS = 2 * P * COMPONENTS * CHANNELS * H * 2 + 2 * P * FEATURES * H


def load_words(nc, words_tile, words, first, count):
    nc.sync.dma_start(
        out=words_tile[:, first : first + count, :].bitcast(I32),
        in_=words[first : first + count].rearrange("g p n t -> p g (n t)").bitcast(I32),
    )


def load_scales(nc, shared, scales):
    count = scales.shape[0]
    for q in range(4):
        nc.sync.dma_start(
            out=shared[32 * q : 32 * q + 4 * count, :].bitcast(I32), in_=scales[:, 4 * q : 4 * q + 4, :].bitcast(I32)
        )


def tile_ryeelman_pa_k_kernel(
    tc,
    invariant_input,
    equivariant_input,
    invariant_hidden,
    equivariant_hidden,
    W_left_words,
    W_left_scales,
    W_right_words,
    W_right_scales,
    W_ii_words,
    W_ii_scales,
    b_ii,
    out,
):
    nc = tc.nc
    with ExitStack() as stack:
        stack.enter_context(tc.manual_schedule())
        keep = stack.enter_context(tc.tile_pool(name="keep", bufs=1))
        work = stack.enter_context(tc.tile_pool(name="work", bufs=2))
        sums = stack.enter_context(tc.psum_pool(name="sums", bufs=1))
        banks = stack.enter_context(tc.psum_pool(name="banks", bufs=1))

        one = keep.tile([P, 1], F32)
        nc.vector.memset(one[:], 1.0)
        warm = keep.tile([P, 2], F32)
        nc.scalar.activation(out=warm[:, 0:1], in_=one[:], func=ACT.Abs_reciprocal_sqrt)

        identity = keep.tile([P, P], F32)
        make_identity(nc, identity[:])

        first_input = keep.tile([P, COMPONENTS], BF16)
        first_hidden = keep.tile([P, COMPONENTS, BLOCK - 1], BF16)
        inv = keep.tile([P, FEATURES], BF16, align_bytes=64)
        bias = keep.tile([P, H], BF16)
        w_words = {}
        w_planes = {}
        for side in SIDES:
            w_words[side] = keep.tile([P, STEPS, PACK * H], U8, align_bytes=64, name="w_words_" + side)
            w_planes[side] = keep.tile([P, STEPS // SHARE, H], U8, align_bytes=64, name="w_planes_" + side)
        ii_words = keep.tile([P, II_PASSES, PACK * H], U8, align_bytes=64)
        ii_planes = keep.tile([P, H], U8, align_bytes=64)
        for plane_tile in (w_planes["left"], w_planes["right"], ii_planes):
            nc.vector.memset(plane_tile[:].bitcast(I32), 0)

        eq = {}

        def load_eq(first, count):
            tile = keep.tile([P, COMPONENTS, count * K_PASS], BF16, align_bytes=64, name="eq_%d" % first)
            for i in range(count):
                eq[first + i] = tile[:, :, K_PASS * i : K_PASS * (i + 1)]
            lo = K_PASS * first
            hi = lo + count * K_PASS
            skip = BLOCK if first == 0 else 0
            if first == ORDER[0]:
                for j in range(COMPONENTS):
                    nc.sync.dma_start(out=tile[:, j, :], in_=equivariant_hidden[:, j, lo - 1 : hi - 1])
            else:
                nc.sync.dma_start(out=tile[:, :, skip:], in_=equivariant_hidden[:, :, lo + skip - 1 : hi - 1])
            if first == 0:
                nc.sync.dma_start(out=first_input[:], in_=equivariant_input)
                nc.sync.dma_start(out=first_hidden[:], in_=equivariant_hidden[:, :, 0 : BLOCK - 1])

        def load_weights(first, count):
            for side, words in zip(SIDES, (W_left_words, W_right_words)):
                load_words(nc, w_words[side], words, first, count)

        def load_weight_scales(g):
            for side, scales in zip(SIDES, (W_left_scales, W_right_scales)):
                load_scales(nc, w_planes[side][:, g, :], scales[SHARE * g : SHARE * (g + 1)])

        for first, count in EQ_LOADS[:2]:
            load_eq(first, count)
        nc.sync.dma_start(out=inv[:, 0 : FEATURES // 2], in_=invariant_input)
        nc.sync.dma_start(out=inv[:, FEATURES // 2 : FEATURES], in_=invariant_hidden)
        for first, count in EQ_LOADS[2:4]:
            load_eq(first, count)
        for i, step in enumerate(ORDER):
            if i % SHARE == 0:
                load_weight_scales(i // SHARE)
            load_weights(step, 1)
            if i % 2 == 0 and i // 2 + 4 < len(EQ_LOADS):
                load_eq(EQ_LOADS[i // 2 + 4][0], EQ_LOADS[i // 2 + 4][1])
        load_scales(nc, ii_planes[:], W_ii_scales)
        load_words(nc, ii_words, W_ii_words, 0, II_PASSES)
        nc.sync.dma_start(out=bias[:], in_=b_ii.partition_broadcast(P))

        acc = {}
        for side in SIDES:
            for j in range(COMPONENTS):
                if (side, j) != ("right", 2):
                    acc[side, j] = sums.tile([P, H], F32, name="acc_%s_%d" % (side, j))

        squares = {}
        partial = {}
        norm = {}
        norm_bank = {}
        rsqrt = {}
        recip = {}
        pair_bank = {}
        small_bank = {}
        xn = {}
        xn_codes = {}
        xn_planes = {}

        def square(i, j):
            x = eq[ORDER[i]]
            if j == 0:
                squares[i] = work.tile([P, COMPONENTS, K_PASS], F32, name="squares", bufs=3)
                if ORDER[i] == 0:
                    nc.vector.tensor_copy(out=x[:, :, 0:1], in_=first_input[:].unsqueeze(2))
                    nc.vector.tensor_copy(out=x[:, :, 1:BLOCK], in_=first_hidden[:])
            sq = squares[i][:, j, :].rearrange("b (t p) -> b t p", t=PACK)
            xj = x[:, j, :].rearrange("b (p t) -> b t p", t=PACK)
            if i == 0 and j == 1:
                nc.vector.tensor_tensor(out=sq, in0=xj, in1=xj, op=ALU.mult)
            else:
                nc.scalar.activation(out=sq, in_=xj, func=ACT.Square)

        def add_two(i):
            partial[i] = work.tile([P, K_PASS], F32, name="partial", bufs=1)
            engine = nc.vector if i in (0, 2) else nc.gpsimd
            engine.tensor_tensor(out=partial[i][:], in0=squares[i][:, 0, :], in1=squares[i][:, 1, :], op=ALU.add)

        def add_third(i):
            norm[i] = work.tile([P, K_PASS], F32, name="norm")
            nc.vector.scalar_tensor_tensor(
                out=norm[i][:],
                in0=partial[i][:],
                scalar=EPSILON,
                in1=squares[i][:, 2, :],
                op0=ALU.add,
                op1=ALU.add,
            )

        def transpose_norm(i):
            norm_bank[i] = banks.tile([P, PACK, P], F32, name="norm_bank", tag="norm")
            for t in range(PACK):
                nc.tensor.transpose(norm_bank[i][:, t, :], norm[i][:, P * t : P * (t + 1)], identity[:])

        def root(i):
            rsqrt[i] = work.tile([P, P, PACK], F32, name="rsqrt")
            nc.scalar.activation(
                out=rsqrt[i][:], in_=norm_bank[i][:].rearrange("p t b -> p b t"), func=ACT.Abs_reciprocal_sqrt
            )

        def root_squared(i):
            recip[i] = work.tile([P, P, PACK], F32, name="recip", bufs=3)
            nc.scalar.activation(out=recip[i][:], in_=rsqrt[i][:], func=ACT.Square)

        def transpose_words(half_banks, words):
            for u in range(2):
                nc.tensor.transpose(half_banks[:, u, :], words[:, u:PASS_WORDS:2], identity[:])

        def transpose_pair(i):
            pair_bank[i] = banks.tile([P, 2, 2, P], F32, name="pair_bank", tag="pair")
            for j in range(2):
                transpose_words(pair_bank[i][:, j], eq[ORDER[i]][:, j, :].bitcast(F32))

        def transpose_small(i):
            small_bank[i] = banks.tile([P, 2, 2, P], F32, name="small_bank", tag="small")
            transpose_words(small_bank[i][:, 0], eq[ORDER[i]][:, 2, :].bitcast(F32))

        def divide(i, j):
            if j == 0:
                xn[i] = work.tile([P, COMPONENTS, P, PACK], BF16, align_bytes=64, name="xn")
            bank = pair_bank[i][:, j] if j < 2 else small_bank[i][:, 0]
            nc.vector.tensor_tensor(
                out=xn[i][:, j].rearrange("p b (u e) -> p b u e", u=2),
                in0=bank.rearrange("p u b -> p (u b)").bitcast(BF16).rearrange("p (u b e) -> p b u e", u=2, e=2),
                in1=recip[i][:].rearrange("p b (u e) -> p b u e", u=2),
                op=ALU.mult,
            )

        def quantise(i):
            xn_codes[i] = keep.tile([P, COMPONENTS, P], U32, align_bytes=64, name="xn_codes_%d" % i)
            xn_planes[i] = keep.tile([P, COMPONENTS, P], U8, align_bytes=64, name="xn_planes_%d" % i)
            for js in (slice(0, 2), slice(2, 3)):
                nc.vector.quantize_mx(
                    out=xn_codes[i][:, js].rearrange("p j b -> p (j b)").bitcast(FP8X4),
                    scales=xn_planes[i][:, js].rearrange("p j b -> p (j b)"),
                    in_=xn[i][:, js].rearrange("p j b t -> p (j b t)"),
                )

        def contract(i, side, j):
            step = ORDER[i]
            nc.tensor.matmul_mx(
                out=acc[side, j][:],
                lhsT=xn_codes[i][:, j, :].bitcast(FP8X4),
                lhsT_scale=xn_planes[i][:, j, :],
                rhs=w_words[side][:, step, :].bitcast(FP8X4),
                rhs_scale=w_planes[side][4 * (step % SHARE) : P, step // SHARE, :],
                start=(i == 0),
                stop=(i == STEPS - 1),
            )

        def contract_open(i):
            for side, j in (("left", 0), ("right", 0), ("left", 1), ("right", 1), ("left", 2)):
                contract(i, side, j)

        right_2 = []

        def sweep(first, last, h):
            for i in range(first, last):
                step = ORDER[i]
                cols = slice(h * H // 2, (h + 1) * H // 2)
                nc.tensor.matmul_mx(
                    out=right_2[h][:],
                    lhsT=xn_codes[i][:, 2, :].bitcast(FP8X4),
                    lhsT_scale=xn_planes[i][:, 2, :],
                    rhs=w_words["right"][:, step, PACK * cols.start : PACK * cols.stop].bitcast(FP8X4),
                    rhs_scale=w_planes["right"][4 * (step % SHARE) : P, step // SHARE, cols],
                    start=(i == 0),
                    stop=(i == STEPS - 1),
                )

        def is_step(i):
            return 0 <= i < STEPS

        inv_bank = acc["left", 0][:].rearrange("p (c u b) -> p c u b", c=II_PASSES, u=2)
        inv_t = keep.tile([P, II_PASSES, P, PACK], BF16, align_bytes=64)
        inv_codes = keep.tile([P, II_PASSES, P], U32, align_bytes=64)
        inv_planes = keep.tile([P, II_PASSES, P], U8, align_bytes=64)

        def transpose_inv():
            for c in range(II_PASSES):
                transpose_words(inv_bank[:, c], inv[:, K_PASS * c : K_PASS * (c + 1)].bitcast(F32))

        def copy_inv():
            nc.vector.tensor_copy(out=inv_t[:].bitcast(F32), in_=inv_bank.rearrange("p c u b -> p c b u"))

        def quantise_inv():
            nc.vector.quantize_mx(
                out=inv_codes[:].rearrange("p c b -> p (c b)").bitcast(FP8X4),
                scales=inv_planes[:].rearrange("p c b -> p (c b)"),
                in_=inv_t[:].rearrange("p c b t -> p (c b t)"),
            )

        def sum_up(i):
            if is_step(i + 2):
                add_third(i + 2)
            if is_step(i + 3):
                add_two(i + 3)

        def invert(i):
            if is_step(i + 4):
                square(i + 4, 0)
                square(i + 4, 1)
            if is_step(i + 2):
                root(i + 2)
            if is_step(i + 4):
                square(i + 4, 2)
            if is_step(i + 2):
                root_squared(i + 2)

        def front(i):
            filling = i <= FILLING
            if i == -2:
                transpose_pair(0)
                transpose_small(0)
                transpose_inv()
            if not filling:
                sum_up(i)
                if FILLING + 1 < i < STEPS - 1:
                    contract_open(i - 1)
                if is_step(i + 2):
                    transpose_norm(i + 2)
                if i == STEPS - 2:
                    sweep(0, 2, 0)
                invert(i)
            if is_step(i):
                divide(i, 0)
                divide(i, 1)
                if is_step(i + 1):
                    transpose_pair(i + 1)
                divide(i, 2)
                if is_step(i + 1):
                    transpose_small(i + 1)
                if i == STEPS - 2:
                    sweep(2, 4, 0)
                quantise(i)
            if filling:
                sum_up(i)
                if is_step(i + 2):
                    transpose_norm(i + 2)
                invert(i)

        for i in range(-4, STEPS - 1):
            if i == STEPS - 2:
                right_2.append(banks.tile([P, H // 2], F32, name="right_2_first", tag="norm"))
            front(i)
            if i == -2:
                copy_inv()
                quantise_inv()
            if 0 <= i <= FILLING:
                contract_open(i)
        contract_open(STEPS - 2)

        nc.scalar.activation(out=warm[:, 1:2], in_=one[:], func=ACT.Tanh)
        sweep(4, SWEEP_AHEAD, 0)
        front(STEPS - 1)
        contract_open(STEPS - 1)
        lin = banks.tile([P, H], F32, name="lin", tag="small")
        for c in range(II_PASSES):
            nc.tensor.matmul_mx(
                out=lin[:],
                lhsT=inv_codes[:, c, :].bitcast(FP8X4),
                lhsT_scale=inv_planes[:, c, :],
                rhs=ii_words[:, c, :].bitcast(FP8X4),
                rhs_scale=ii_planes[4 * c : P, :],
                start=(c == 0),
                stop=(c == II_PASSES - 1),
            )
        sweep(SWEEP_AHEAD, STEPS, 0)
        right_2.append(banks.tile([P, H // 2], F32, name="right_2_second", tag="pair"))
        sweep(0, STEPS, 1)

        left = []
        product = []
        for j in range(COMPONENTS):
            left.append(keep.tile([P, H], F32, name="left_%d" % j))
            nc.scalar.copy(out=left[j][:], in_=acc["left", j][:])
            product.append(keep.tile([P, H], F32, name="product_%d" % j))
        def multiply(j):
            nc.vector.tensor_tensor(out=product[j][:], in0=left[j][:], in1=acc["right", j][:], op=ALU.mult)

        lin_b = keep.tile([P, H], F32)
        partial_sum = keep.tile([P, H], F32)
        total = keep.tile([P, H], F32)
        final_sum = keep.tile([P, H], F32)
        result = keep.tile([P, H], F32)
        halves = (slice(0, H // 2), slice(H // 2, H))

        def multiply_half(h):
            nc.vector.tensor_tensor(out=product[2][:, halves[h]], in0=left[2][:, halves[h]], in1=right_2[h][:], op=ALU.mult)

        def finish_half(h):
            cols = halves[h]
            nc.vector.tensor_tensor(out=final_sum[:, cols], in0=total[:, cols], in1=product[2][:, cols], op=ALU.add)
            nc.scalar.activation(out=result[:, cols], in_=final_sum[:, cols], func=ACT.Tanh)
            nc.sync.dma_start(out=out[:, cols], in_=result[:, cols])

        multiply(0)
        nc.vector.tensor_tensor(out=lin_b[:], in0=lin[:], in1=bias[:], op=ALU.add)
        multiply(1)
        nc.vector.tensor_tensor(out=partial_sum[:], in0=lin_b[:], in1=product[0][:], op=ALU.add)
        multiply_half(0)
        nc.vector.tensor_tensor(out=total[:], in0=partial_sum[:], in1=product[1][:], op=ALU.add)
        finish_half(0)
        multiply_half(1)
        finish_half(1)
